import numpy as np
import ml_dtypes


def mxq(x, axis, fmt="e4m3"):
    dtype, down = {"e4m3": (ml_dtypes.float8_e4m3fn, 7), "e5m2": (ml_dtypes.float8_e5m2, 14)}[fmt]
    v = np.moveaxis(np.asarray(x, np.float32).astype(ml_dtypes.bfloat16).astype(np.float64), axis, -1)
    blocks = v.reshape(v.shape[:-1] + (-1, 32))
    amax = np.abs(blocks).max(-1, keepdims=True)
    byte = np.maximum(np.where(amax > 0, np.frexp(amax)[1] - 1 + 127, 0) - down, 1)
    scale = np.exp2(byte - 127.0)
    codes = (blocks / scale).astype(np.float32).astype(dtype).astype(np.float64)
    return np.moveaxis((codes * scale).reshape(v.shape), -1, axis)


WIDE = False


def mx_kscale(k):
    if not WIDE:
        return np.ones(k)
    levels = np.array([10, -10, 5, -5, 0])
    if k % 512:
        return np.exp2(np.random.permutation(np.resize(levels, k // 32))).repeat(32)
    a = np.empty((k // 512, 16))
    for p in range(k // 512):
        a[p, :8] = np.random.permutation(np.resize(levels, 8))
        for g in range(8):
            far = levels[np.abs(levels - a[p, g]) >= 10]
            a[p, g + 8] = far[np.random.randint(len(far))]
    return np.exp2(a.ravel()).repeat(32)


BF16 = ml_dtypes.bfloat16


def bf(x):
    return np.asarray(x, np.float32).astype(BF16)


def f64(x):
    return np.asarray(x).astype(np.float64)


B, C, PS, G, E = 24, 3, 64, 4, 512
NP = G * G
K2 = 2 * E


def setup_inputs():
    s = mx_kscale(K2)[:E]
    t = mx_kscale(K2)[:E]
    ss = np.concatenate([s, s])
    tt = np.concatenate([t, t])
    return {"tok": bf(np.random.standard_normal((B, NP, E)) * s),
            "corr_w": bf(np.random.standard_normal((E, K2)) / np.sqrt(K2) * t[:, None] / ss[None, :]),
            "corr_b": bf(np.random.standard_normal(E) * 0.3 * t),
            "cross_w": bf(np.random.standard_normal((E, K2)) / np.sqrt(K2) / tt[None, :]),
            "cross_b": bf(np.random.standard_normal(E) * 0.3)}


def reference(tok, corr_w, corr_b, cross_w, cross_b):
    xc = f64(tok)
    a = np.broadcast_to(xc[:, :, None, :], (B, NP, NP, E))
    b = np.broadcast_to(xc[:, None, :, :], (B, NP, NP, E))
    cart = np.concatenate([a, b], axis=-1)
    h = (mxq(cart, 3, "e4m3") @ mxq(f64(corr_w), 1, "e4m3").T) + f64(corr_b)
    h = h.reshape(B, NP, NP // 2, K2)
    return (mxq(h, 3, "e4m3") @ mxq(f64(cross_w), 1, "e4m3").T) + f64(cross_b)

@@ -1,0 +1,296 @@
+from contextlib import ExitStack
+
+import concourse.mybir as mybir
+from concourse.masks import make_identity
+
+F32 = mybir.dt.float32
+BF16 = mybir.dt.bfloat16
+U32 = mybir.dt.uint32
+U8 = mybir.dt.uint8
+FP8X4 = mybir.dt.float8_e4m3fn_x4
+ADD = mybir.AluOpType.add
+IDENTITY = mybir.ActivationFunctionType.Identity
+
+P = 128
+IMAGES = 24
+TOKENS = 16
+PAIRS = TOKENS // 2
+E = 512
+E_TILES = E // P
+PACK = 4
+K_PASS = P * PACK
+TOKEN_TILES = IMAGES * TOKENS // P
+IMAGES_PER_TILE = P // TOKENS
+GROUP = 2
+GROUP_ROWS = GROUP * P
+GROUPS = IMAGES // GROUP
+VECTOR_TILES = 2
+VECTOR_GROUPS = VECTOR_TILES * IMAGES_PER_TILE // GROUP
+LAG = 2
+
+FLOPS = 2 * IMAGES * TOKENS * TOKENS * 2 * E * E + 2 * IMAGES * TOKENS * PAIRS * 2 * E * E
+
+
+def tile_simplemodel_pb_kernel(tc, tok, corr_w, corr_b, cross_w, cross_b, out):
+    nc = tc.nc
+    tok_rows = tok.flatten_outer_dims()
+    out_rows = out.flatten_outer_dims()
+
+    with ExitStack() as stack:
+        stack.enter_context(tc.manual_schedule())
+        keep = stack.enter_context(tc.tile_pool(name="keep", bufs=1))
+        h_pool = stack.enter_context(tc.tile_pool(name="h", bufs=4))
+        code_pool = stack.enter_context(tc.tile_pool(name="codes", bufs=6))
+        out_pool = stack.enter_context(tc.tile_pool(name="o", bufs=4))
+        psum_keep = stack.enter_context(tc.psum_pool(name="psum_keep", bufs=1))
+        psum = stack.enter_context(tc.psum_pool(name="psum", bufs=4))
+
+        tok_sb = keep.tile([P, TOKEN_TILES * E], BF16)
+        nc.sync.dma_start(
+            out=tok_sb[:].rearrange("p (n k) -> p n k", n=TOKEN_TILES),
+            in_=tok_rows.rearrange("(n p) k -> p n k", p=P),
+        )
+        w1_sb = keep.tile([P, PACK * 2 * E], BF16)
+        w1_dram = corr_w.rearrange("(p t) k -> t p k", t=PACK)
+        for t in range(PACK):
+            nc.sync.dma_start(
+                out=w1_sb[:, t * 2 * E : (t + 1) * 2 * E], in_=w1_dram[t]
+            )
+        w2_sb = keep.tile([P, E_TILES * 2 * E], BF16)
+        w2_dram = cross_w.rearrange("(n p) k -> p n k", p=P)
+        for half in range(2):
+            nc.sync.dma_start(
+                out=w2_sb[:, half * 4 * E : (half + 1) * 4 * E].rearrange("p (n k) -> p n k", n=2),
+                in_=w2_dram[:, 2 * half : 2 * half + 2, :],
+            )
+        bias1 = keep.tile([P, PACK], BF16)
+        nc.scalar.dma_start(out=bias1[:], in_=corr_b.rearrange("(p t) -> p t", t=PACK))
+        bias2_bf = keep.tile([P, E_TILES], BF16)
+        with nc.allow_non_contiguous_dma(reason="512 bias values, one to a partition and tile"):
+            nc.scalar.dma_start(out=bias2_bf[:], in_=cross_b.rearrange("(n p) -> p n", p=P))
+
+        ident = keep.tile([P, P], F32)
+        make_identity(nc, ident[:])
+        table_loaded = keep.tile([P, 1], F32)
+        nc.scalar.activation(out=table_loaded[:], in_=ident[:, 0:1], func=IDENTITY)
+
+        tok_grouped = keep.tile([P, TOKEN_TILES * P * PACK], BF16, align_bytes=64)
+        tok_codes = keep.tile([P, TOKEN_TILES * P], U32, align_bytes=64)
+        tok_scales = keep.tile([P, TOKEN_TILES * P], U8, align_bytes=64)
+        w1_grouped = keep.tile([P, PACK * 2 * K_PASS], BF16, align_bytes=64)
+        w1_codes = keep.tile([P, PACK * 2 * P], U32, align_bytes=64)
+        w1_scales = keep.tile([P, PACK * 2 * P], U8, align_bytes=64)
+        w2_grouped = keep.tile([P, 2 * E * PACK], BF16, align_bytes=64)
+        w2_codes = keep.tile([P, 2 * E], U32, align_bytes=64)
+        w2_scales = keep.tile([P, 2 * E], U8, align_bytes=64)
+        bias2 = keep.tile([P, E_TILES], F32)
+        second = keep.tile([P, IMAGES, 2, PAIRS, PACK], F32)
+        first_sbuf = keep.tile([P, P, PACK], F32)
+        first_psum = {}
+        for n in range(VECTOR_TILES):
+            first_psum[n] = psum_keep.tile([P, PACK, P], F32, name="first_psum%d" % n)
+
+        def transpose_words(words, first_word, count):
+            bank = psum.tile([P, count, P], F32, tag="bank")
+            for s in range(count):
+                begin = first_word + (s // 2) * 2 * P
+                nc.tensor.transpose(
+                    bank[:, s, :], words[:, begin + s % 2 : begin + 2 * P : 2], ident[:]
+                )
+            return bank
+
+        tok_words = tok_sb[:].bitcast(F32)
+
+        def prepare_tokens(n):
+            bank = transpose_words(tok_words, n * 2 * P, 2)
+            nc.scalar.copy(
+                out=tok_grouped[:, n * K_PASS : (n + 1) * K_PASS]
+                .bitcast(F32)
+                .rearrange("q (r u) -> q r u", u=2),
+                in_=bank[:].rearrange("q u r -> q r u"),
+            )
+            nc.vector.quantize_mx(
+                out=tok_codes[:, n * P : (n + 1) * P].bitcast(FP8X4),
+                scales=tok_scales[:, n * P : (n + 1) * P],
+                in_=tok_grouped[:, n * K_PASS : (n + 1) * K_PASS],
+            )
+
+        def first_matmul(product, half, n, t):
+            w_cols = slice((2 * t + half) * P, (2 * t + half + 1) * P)
+            t_cols = slice(n * P, (n + 1) * P)
+            nc.tensor.matmul_mx(
+                out=product[:, t, :],
+                lhsT=w1_codes[:, w_cols].bitcast(FP8X4),
+                lhsT_scale=w1_scales[:, w_cols],
+                rhs=tok_codes[:, t_cols].bitcast(FP8X4),
+                rhs_scale=tok_scales[:, t_cols],
+                start=True,
+                stop=True,
+            )
+
+        def second_to_sbuf(product, n):
+            for c in range(2):
+                nc.vector.tensor_tensor(
+                    out=second[:, n * IMAGES_PER_TILE : (n + 1) * IMAGES_PER_TILE, c],
+                    in0=product[:].rearrange("q t (b m c) -> q c b m t", m=PAIRS, c=2)[:, c],
+                    in1=bias1[:]
+                    .unsqueeze(1)
+                    .unsqueeze(1)
+                    .to_broadcast([P, IMAGES_PER_TILE, PAIRS, PACK]),
+                    op=ADD,
+                )
+
+        def prepare_corr_w(t):
+            bank = transpose_words(w1_words, t * E, 4)
+            nc.scalar.copy(
+                out=w1_grouped[:, t * 2 * K_PASS : (t + 1) * 2 * K_PASS]
+                .bitcast(F32)
+                .rearrange("q (h r u) -> q h r u", h=2, u=2),
+                in_=bank[:].rearrange("q (h u) r -> q h r u", u=2),
+            )
+            nc.vector.quantize_mx(
+                out=w1_codes[:, t * 2 * P : (t + 1) * 2 * P].bitcast(FP8X4),
+                scales=w1_scales[:, t * 2 * P : (t + 1) * 2 * P],
+                in_=w1_grouped[:, t * 2 * K_PASS : (t + 1) * 2 * K_PASS],
+            )
+
+        w1_words = w1_sb[:].bitcast(F32)
+        second_psum0 = psum.tile([P, PACK, P], F32, tag="product", bufs=2)
+        prepare_tokens(0)
+        for t in range(PACK):
+            prepare_corr_w(t)
+            if t >= LAG:
+                first_matmul(second_psum0, 1, 0, t - LAG)
+                first_matmul(first_psum[0], 0, 0, t - LAG)
+        prepare_tokens(2)
+        prepare_tokens(1)
+        nc.scalar.activation(out=bias2[:], in_=bias2_bf[:], func=IDENTITY)
+        for t in range(PACK - LAG, PACK):
+            first_matmul(second_psum0, 1, 0, t)
+            first_matmul(first_psum[0], 0, 0, t)
+        second_to_sbuf(second_psum0, 0)
+
+        first_psum2 = psum.tile([P, PACK, P], F32, tag="product", bufs=2)
+        for t in range(PACK):
+            first_matmul(first_psum2, 0, 2, t)
+        nc.scalar.copy(out=first_sbuf[:], in_=first_psum2[:].rearrange("q t r -> q r t"))
+        second_psum2 = psum.tile([P, PACK, P], F32, tag="product", bufs=2)
+        for t in range(PACK):
+            first_matmul(second_psum2, 1, 2, t)
+        second_to_sbuf(second_psum2, 2)
+
+        w2_words = w2_sb[:].bitcast(F32)
+        for n in range(E_TILES):
+            bank = transpose_words(w2_words, n * E, 4)
+            nc.scalar.copy(
+                out=w2_grouped[:]
+                .bitcast(F32)
+                .rearrange("q (c n r u) -> q n c r u", c=2, n=E_TILES, u=2)[:, n],
+                in_=bank[:].rearrange("q (c u) r -> q c r u", u=2),
+            )
+
+        second_psum1 = psum.tile([P, PACK, P], F32, tag="product", bufs=2)
+        for t in range(PACK):
+            first_matmul(second_psum1, 1, 1, t)
+            first_matmul(first_psum[1], 0, 1, t)
+
+        full = [P, GROUP, TOKENS, PAIRS, PACK]
+
+        def add_half(g, c):
+            b0 = g * GROUP
+            t0 = (b0 % IMAGES_PER_TILE) * TOKENS
+            if g < VECTOR_GROUPS:
+                engine = nc.vector
+                h_grouped = h_pool.tile([P, GROUP, P * PACK], BF16, align_bytes=64, tag="h_vector")
+                bank = first_psum[b0 // IMAGES_PER_TILE]
+                first = bank[:, :, t0 : t0 + GROUP * TOKENS].rearrange("q t (b i) -> q b i t", b=GROUP)
+            else:
+                engine = nc.gpsimd
+                h_grouped = h_pool.tile(
+                    [P, GROUP, P * PACK], BF16, align_bytes=64, tag="h_gpsimd", bufs=1
+                )
+                first = first_sbuf[:, t0 : t0 + GROUP * TOKENS, :].rearrange(
+                    "q (b i) t -> q b i t", b=GROUP
+                )
+            engine.tensor_tensor(
+                out=h_grouped[:].rearrange("q b (i m t) -> q b i m t", i=TOKENS, m=PAIRS),
+                in0=first.unsqueeze(3).to_broadcast(full),
+                in1=second[:, b0 : b0 + GROUP, c].unsqueeze(2).to_broadcast(full),
+                op=ADD,
+            )
+            return h_grouped
+
+        def quantise_half(h_grouped):
+            h_codes = code_pool.tile([P, GROUP_ROWS], U32, align_bytes=64)
+            h_scales = code_pool.tile([P, GROUP_ROWS], U8, align_bytes=64)
+            nc.vector.quantize_mx(
+                out=h_codes[:].bitcast(FP8X4),
+                scales=h_scales[:],
+                in_=h_grouped[:].rearrange("q b x -> q (b x)"),
+            )
+            return h_codes, h_scales
+
+        def multiply_group(halves):
+            out_t = out_pool.tile([P, E_TILES, GROUP_ROWS], F32)
+            for pair in range(E_TILES // 2):
+                acc = psum.tile([P, 2, GROUP_ROWS], F32, tag="bank")
+                for s in range(2):
+                    n = 2 * pair + s
+                    for c in range(2):
+                        h_codes, h_scales = halves[c]
+                        w_cols = slice(c * E + n * P, c * E + (n + 1) * P)
+                        nc.tensor.matmul_mx(
+                            out=acc[:, s, :],
+                            lhsT=w2_codes[:, w_cols].bitcast(FP8X4),
+                            lhsT_scale=w2_scales[:, w_cols],
+                            rhs=h_codes[:].bitcast(FP8X4),
+                            rhs_scale=h_scales[:],
+                            start=(c == 0),
+                            stop=(c == 1),
+                        )
+                for s in range(2):
+                    n = 2 * pair + s
+                    nc.scalar.activation(
+                        out=out_t[:, n, :],
+                        in_=acc[:, s, :],
+                        func=IDENTITY,
+                        bias=bias2[:, n : n + 1],
+                        scale=1.0,
+                    )
+            return out_t
+
+        def store_group(g, out_t, copy):
+            for b in range(GROUP):
+                back = psum.tile([P, E_TILES, P], F32, tag="bank")
+                for n in range(E_TILES):
+                    nc.tensor.transpose(back[:, n, :], out_t[:, n, b * P : (b + 1) * P], ident[:])
+                result = out_pool.tile([P, E], F32)
+                copy(out=result[:], in_=back[:].rearrange("r n e -> r (n e)"))
+                row0 = (g * GROUP + b) * P
+                nc.sync.dma_start(out=out_rows[row0 : row0 + P, :], in_=result[:])
+
+        gpsimd_halves = []
+        previous = None
+        for k in range(VECTOR_GROUPS):
+            from_gpsimd = add_half(VECTOR_GROUPS + k // 2, k % 2)
+            from_vector = [add_half(k, c) for c in range(2)]
+            if k == 0:
+                for c in range(2):
+                    nc.vector.quantize_mx(
+                        out=w2_codes[:, c * E : (c + 1) * E].bitcast(FP8X4),
+                        scales=w2_scales[:, c * E : (c + 1) * E],
+                        in_=w2_grouped[:, c * E * PACK : (c + 1) * E * PACK],
+                    )
+            ready = [(k, [quantise_half(h_grouped) for h_grouped in from_vector])]
+            gpsimd_halves.append(quantise_half(from_gpsimd))
+            if k % 2 == 1:
+                ready.append((VECTOR_GROUPS + k // 2, gpsimd_halves[k - 1 : k + 1]))
+            if k == 0:
+                second_to_sbuf(second_psum1, 1)
+            copy = nc.vector.tensor_copy if k == VECTOR_GROUPS - 1 else nc.scalar.copy
+            for g, halves in ready:
+                out_t = multiply_group(halves)
+                if previous is not None:
+                    store_group(previous[0], previous[1], copy)
+                previous = (g, out_t)
+        store_group(previous[0], previous[1], nc.vector.tensor_copy)

@@ -23,10 +23,8 @@ TOKEN_TILES = IMAGES * TOKENS // P
 IMAGES_PER_TILE = P // TOKENS
 GROUP = 2
 GROUP_ROWS = GROUP * P
-GROUPS = IMAGES // GROUP
 VECTOR_TILES = 2
 VECTOR_GROUPS = VECTOR_TILES * IMAGES_PER_TILE // GROUP
-LAG = 2
 
 FLOPS = 2 * IMAGES * TOKENS * TOKENS * 2 * E * E + 2 * IMAGES * TOKENS * PAIRS * 2 * E * E
 
@@ -43,19 +41,19 @@ def tile_simplemodel_pb_kernel(tc, tok, corr_w, corr_b, cross_w, cross_b, out):
         code_pool = stack.enter_context(tc.tile_pool(name="codes", bufs=6))
         out_pool = stack.enter_context(tc.tile_pool(name="o", bufs=4))
         psum_keep = stack.enter_context(tc.psum_pool(name="psum_keep", bufs=1))
-        psum = stack.enter_context(tc.psum_pool(name="psum", bufs=4))
+        psum = stack.enter_context(tc.psum_pool(name="psum", bufs=6))
 
         tok_sb = keep.tile([P, TOKEN_TILES * E], BF16)
-        nc.sync.dma_start(
-            out=tok_sb[:].rearrange("p (n k) -> p n k", n=TOKEN_TILES),
-            in_=tok_rows.rearrange("(n p) k -> p n k", p=P),
-        )
+        tok_view = tok_sb[:].rearrange("p (n k) -> p n k", n=TOKEN_TILES)
+        tok_dram = tok_rows.rearrange("(n p) k -> p n k", p=P)
+        nc.sync.dma_start(out=tok_view[:, 0:1], in_=tok_dram[:, 0:1])
         w1_sb = keep.tile([P, PACK * 2 * E], BF16)
         w1_dram = corr_w.rearrange("(p t) k -> t p k", t=PACK)
         for t in range(PACK):
             nc.sync.dma_start(
                 out=w1_sb[:, t * 2 * E : (t + 1) * 2 * E], in_=w1_dram[t]
             )
+        nc.sync.dma_start(out=tok_view[:, 1:], in_=tok_dram[:, 1:])
         w2_sb = keep.tile([P, E_TILES * 2 * E], BF16)
         w2_dram = cross_w.rearrange("(n p) k -> p n k", p=P)
         for half in range(2):
@@ -63,16 +61,15 @@ def tile_simplemodel_pb_kernel(tc, tok, corr_w, corr_b, cross_w, cross_b, out):
                 out=w2_sb[:, half * 4 * E : (half + 1) * 4 * E].rearrange("p (n k) -> p n k", n=2),
                 in_=w2_dram[:, 2 * half : 2 * half + 2, :],
             )
+        bias2_row = keep.tile([P, E], BF16)
+        nc.sync.dma_start(out=bias2_row[:], in_=cross_b.partition_broadcast(P))
         bias1 = keep.tile([P, PACK], BF16)
         nc.scalar.dma_start(out=bias1[:], in_=corr_b.rearrange("(p t) -> p t", t=PACK))
-        bias2_bf = keep.tile([P, E_TILES], BF16)
-        with nc.allow_non_contiguous_dma(reason="512 bias values, one to a partition and tile"):
-            nc.scalar.dma_start(out=bias2_bf[:], in_=cross_b.rearrange("(n p) -> p n", p=P))
 
         ident = keep.tile([P, P], F32)
         make_identity(nc, ident[:])
-        table_loaded = keep.tile([P, 1], F32)
-        nc.scalar.activation(out=table_loaded[:], in_=ident[:, 0:1], func=IDENTITY)
+        unit = keep.tile([P, 1], BF16)
+        nc.scalar.activation(out=unit[:], in_=ident[:, 0:1], func=IDENTITY)
 
         tok_grouped = keep.tile([P, TOKEN_TILES * P * PACK], BF16, align_bytes=64)
         tok_codes = keep.tile([P, TOKEN_TILES * P], U32, align_bytes=64)
@@ -86,13 +83,10 @@ def tile_simplemodel_pb_kernel(tc, tok, corr_w, corr_b, cross_w, cross_b, out):
         bias2 = keep.tile([P, E_TILES], F32)
         second = keep.tile([P, IMAGES, 2, PAIRS, PACK], F32)
         first_sbuf = keep.tile([P, P, PACK], F32)
-        first_psum = {}
-        for n in range(VECTOR_TILES):
-            first_psum[n] = psum_keep.tile([P, PACK, P], F32, name="first_psum%d" % n)
 
-        def transpose_words(words, first_word, count):
-            bank = psum.tile([P, count, P], F32, tag="bank")
-            for s in range(count):
+        def transpose_words(words, first_word, passes):
+            bank = psum.tile([P, 2 * passes, P], F32, tag="bank")
+            for s in range(2 * passes):
                 begin = first_word + (s // 2) * 2 * P
                 nc.tensor.transpose(
                     bank[:, s, :], words[:, begin + s % 2 : begin + 2 * P : 2], ident[:]
@@ -100,20 +94,62 @@ def tile_simplemodel_pb_kernel(tc, tok, corr_w, corr_b, cross_w, cross_b, out):
             return bank
 
         tok_words = tok_sb[:].bitcast(F32)
+        w1_words = w1_sb[:].bitcast(F32)
+        w2_words = w2_sb[:].bitcast(F32)
 
-        def prepare_tokens(n):
-            bank = transpose_words(tok_words, n * 2 * P, 2)
+        def transpose_tokens(n):
+            bank = transpose_words(tok_words, n * 2 * P, 1)
             nc.scalar.copy(
                 out=tok_grouped[:, n * K_PASS : (n + 1) * K_PASS]
                 .bitcast(F32)
                 .rearrange("q (r u) -> q r u", u=2),
                 in_=bank[:].rearrange("q u r -> q r u"),
             )
+
+        def quantise_tokens(n):
             nc.vector.quantize_mx(
                 out=tok_codes[:, n * P : (n + 1) * P].bitcast(FP8X4),
                 scales=tok_scales[:, n * P : (n + 1) * P],
                 in_=tok_grouped[:, n * K_PASS : (n + 1) * K_PASS],
             )
+
+        def transpose_corr_w(t, half, halves, copy):
+            bank = transpose_words(w1_words, t * E + half * 2 * P, halves)
+            start = (2 * t + half) * K_PASS
+            copy(
+                out=w1_grouped[:, start : start + halves * K_PASS]
+                .bitcast(F32)
+                .rearrange("q (h r u) -> q h r u", h=halves, u=2),
+                in_=bank[:].rearrange("q (h u) r -> q h r u", u=2),
+            )
+
+        def quantise_corr_w(t, half, halves):
+            start = (2 * t + half) * P
+            stop = start + halves * P
+            nc.vector.quantize_mx(
+                out=w1_codes[:, start:stop].bitcast(FP8X4),
+                scales=w1_scales[:, start:stop],
+                in_=w1_grouped[:, start * PACK : stop * PACK],
+            )
+
+        def transpose_cross_w(n):
+            bank = transpose_words(w2_words, n * E, 2)
+            nc.scalar.copy(
+                out=w2_grouped[:]
+                .bitcast(F32)
+                .rearrange("q (c n r u) -> q n c r u", c=2, n=E_TILES, u=2)[:, n],
+                in_=bank[:].rearrange("q (c u) r -> q c r u", u=2),
+            )
+
+        def quantise_cross_w(pair):
+            for c in range(2):
+                start = c * E + pair * 2 * P
+                stop = start + 2 * P
+                nc.vector.quantize_mx(
+                    out=w2_codes[:, start:stop].bitcast(FP8X4),
+                    scales=w2_scales[:, start:stop],
+                    in_=w2_grouped[:, start * PACK : stop * PACK],
+                )
 
         def first_matmul(product, half, n, t):
             w_cols = slice((2 * t + half) * P, (2 * t + half + 1) * P)
@@ -128,71 +164,51 @@ def tile_simplemodel_pb_kernel(tc, tok, corr_w, corr_b, cross_w, cross_b, out):
                 stop=True,
             )
 
-        def second_to_sbuf(product, n):
+        def second_to_sbuf(product, n, first_image, images):
+            tokens = slice(first_image * TOKENS, (first_image + images) * TOKENS)
+            b0 = n * IMAGES_PER_TILE + first_image
             for c in range(2):
                 nc.vector.tensor_tensor(
-                    out=second[:, n * IMAGES_PER_TILE : (n + 1) * IMAGES_PER_TILE, c],
-                    in0=product[:].rearrange("q t (b m c) -> q c b m t", m=PAIRS, c=2)[:, c],
-                    in1=bias1[:]
-                    .unsqueeze(1)
-                    .unsqueeze(1)
-                    .to_broadcast([P, IMAGES_PER_TILE, PAIRS, PACK]),
+                    out=second[:, b0 : b0 + images, c],
+                    in0=product[:, :, tokens].rearrange("q t (b m c) -> q c b m t", m=PAIRS, c=2)[:, c],
+                    in1=bias1[:].unsqueeze(1).unsqueeze(1).to_broadcast([P, images, PAIRS, PACK]),
                     op=ADD,
                 )
 
-        def prepare_corr_w(t):
-            bank = transpose_words(w1_words, t * E, 4)
-            nc.scalar.copy(
-                out=w1_grouped[:, t * 2 * K_PASS : (t + 1) * 2 * K_PASS]
-                .bitcast(F32)
-                .rearrange("q (h r u) -> q h r u", h=2, u=2),
-                in_=bank[:].rearrange("q (h u) r -> q h r u", u=2),
-            )
-            nc.vector.quantize_mx(
-                out=w1_codes[:, t * 2 * P : (t + 1) * 2 * P].bitcast(FP8X4),
-                scales=w1_scales[:, t * 2 * P : (t + 1) * 2 * P],
-                in_=w1_grouped[:, t * 2 * K_PASS : (t + 1) * 2 * K_PASS],
-            )
-
-        w1_words = w1_sb[:].bitcast(F32)
-        second_psum0 = psum.tile([P, PACK, P], F32, tag="product", bufs=2)
-        prepare_tokens(0)
-        for t in range(PACK):
-            prepare_corr_w(t)
-            if t >= LAG:
-                first_matmul(second_psum0, 1, 0, t - LAG)
-                first_matmul(first_psum[0], 0, 0, t - LAG)
-        prepare_tokens(2)
-        prepare_tokens(1)
-        nc.scalar.activation(out=bias2[:], in_=bias2_bf[:], func=IDENTITY)
-        for t in range(PACK - LAG, PACK):
+        first_psum = {}
+        first_psum[0] = psum_keep.tile([P, PACK, P], F32, name="first_psum0")
+        second_psum0 = psum_keep.tile([P, PACK, P], F32, name="second_psum0", tag="shared")
+        transpose_tokens(0)
+        quantise_tokens(0)
+        for t in range(3):
+            transpose_corr_w(t, 0, 2, nc.scalar.copy)
+            quantise_corr_w(t, 0, 2)
+        first_matmul(second_psum0, 1, 0, 0)
+        first_matmul(first_psum[0], 0, 0, 0)
+        transpose_corr_w(3, 1, 1, nc.scalar.copy)
+        transpose_corr_w(3, 0, 1, nc.vector.tensor_copy)
+        quantise_corr_w(3, 1, 1)
+        quantise_corr_w(3, 0, 1)
+        for t in range(1, 3):
             first_matmul(second_psum0, 1, 0, t)
             first_matmul(first_psum[0], 0, 0, t)
-        second_to_sbuf(second_psum0, 0)
+        transpose_tokens(2)
+        transpose_tokens(1)
+        quantise_tokens(2)
+        first_matmul(second_psum0, 1, 0, 3)
+        first_matmul(first_psum[0], 0, 0, 3)
+        second_to_sbuf(second_psum0, 0, 0, GROUP)
 
-        first_psum2 = psum.tile([P, PACK, P], F32, tag="product", bufs=2)
-        for t in range(PACK):
-            first_matmul(first_psum2, 0, 2, t)
-        nc.scalar.copy(out=first_sbuf[:], in_=first_psum2[:].rearrange("q t r -> q r t"))
-        second_psum2 = psum.tile([P, PACK, P], F32, tag="product", bufs=2)
+        transpose_cross_w(0)
+        second_psum2 = psum.tile([P, PACK, P], F32, tag="bank")
+        first_psum2 = psum.tile([P, PACK, P], F32, tag="bank")
         for t in range(PACK):
             first_matmul(second_psum2, 1, 2, t)
-        second_to_sbuf(second_psum2, 2)
-
-        w2_words = w2_sb[:].bitcast(F32)
-        for n in range(E_TILES):
-            bank = transpose_words(w2_words, n * E, 4)
-            nc.scalar.copy(
-                out=w2_grouped[:]
-                .bitcast(F32)
-                .rearrange("q (c n r u) -> q n c r u", c=2, n=E_TILES, u=2)[:, n],
-                in_=bank[:].rearrange("q (c u) r -> q c r u", u=2),
-            )
-
-        second_psum1 = psum.tile([P, PACK, P], F32, tag="product", bufs=2)
-        for t in range(PACK):
-            first_matmul(second_psum1, 1, 1, t)
-            first_matmul(first_psum[1], 0, 1, t)
+            first_matmul(first_psum2, 0, 2, t)
+        nc.scalar.copy(out=first_sbuf[:], in_=first_psum2[:].rearrange("q t r -> q r t"))
+        second_to_sbuf(second_psum2, 2, 0, GROUP)
+        for n in range(1, E_TILES):
+            transpose_cross_w(n)
 
         full = [P, GROUP, TOKENS, PAIRS, PACK]
 
@@ -259,38 +275,93 @@ def tile_simplemodel_pb_kernel(tc, tok, corr_w, corr_b, cross_w, cross_b, out):
                     )
             return out_t
 
-        def store_group(g, out_t, copy):
+        def store_group(g, out_t):
             for b in range(GROUP):
                 back = psum.tile([P, E_TILES, P], F32, tag="bank")
                 for n in range(E_TILES):
                     nc.tensor.transpose(back[:, n, :], out_t[:, n, b * P : (b + 1) * P], ident[:])
                 result = out_pool.tile([P, E], F32)
-                copy(out=result[:], in_=back[:].rearrange("r n e -> r (n e)"))
+                nc.scalar.copy(out=result[:], in_=back[:].rearrange("r n e -> r (n e)"))
+                row0 = (g * GROUP + b) * P
+                nc.sync.dma_start(out=out_rows[row0 : row0 + P, :], in_=result[:])
+
+        def multiply_direct(halves):
+            banks = []
+            for b in range(GROUP):
+                acc = psum.tile([P, E], F32, tag="bank")
+                for c in range(2):
+                    h_codes, h_scales = halves[c]
+                    nc.tensor.matmul_mx(
+                        out=acc[:],
+                        lhsT=h_codes[:, b * P : (b + 1) * P].bitcast(FP8X4),
+                        lhsT_scale=h_scales[:, b * P : (b + 1) * P],
+                        rhs=w2_codes[:, c * E : (c + 1) * E].bitcast(FP8X4),
+                        rhs_scale=w2_scales[:, c * E : (c + 1) * E],
+                        start=(c == 0),
+                        stop=(c == 1),
+                    )
+                banks.append(acc)
+            return banks
+
+        def store_direct(g, banks):
+            for b in range(GROUP):
+                result = out_pool.tile([P, E], F32, tag="direct")
+                nc.vector.tensor_tensor(out=result[:], in0=banks[b][:], in1=bias2_row[:], op=ADD)
                 row0 = (g * GROUP + b) * P
                 nc.sync.dma_start(out=out_rows[row0 : row0 + P, :], in_=result[:])
 
         gpsimd_halves = []
-        previous = None
+        multiplied = []
         for k in range(VECTOR_GROUPS):
+            last_round = k == VECTOR_GROUPS - 1
             from_gpsimd = add_half(VECTOR_GROUPS + k // 2, k % 2)
             from_vector = [add_half(k, c) for c in range(2)]
+            if not last_round:
+                for g, out_t in multiplied:
+                    store_group(g, out_t)
+                multiplied = []
             if k == 0:
-                for c in range(2):
-                    nc.vector.quantize_mx(
-                        out=w2_codes[:, c * E : (c + 1) * E].bitcast(FP8X4),
-                        scales=w2_scales[:, c * E : (c + 1) * E],
-                        in_=w2_grouped[:, c * E * PACK : (c + 1) * E * PACK],
+                quantise_cross_w(0)
+            if last_round:
+                gpsimd_halves.append(quantise_half(from_gpsimd))
+                halves = [quantise_half(h_grouped) for h_grouped in from_vector]
+                direct = [
+                    (VECTOR_GROUPS + k // 2, multiply_direct(gpsimd_halves[k - 1 : k + 1])),
+                    (k, multiply_direct(halves)),
+                ]
+                for g, out_t in multiplied:
+                    store_group(g, out_t)
+                for g, banks in direct:
+                    store_direct(g, banks)
+            else:
+                halves = [quantise_half(h_grouped) for h_grouped in from_vector]
+                if k == 0:
+                    quantise_cross_w(1)
+                gpsimd_halves.append(quantise_half(from_gpsimd))
+                if k == 0:
+                    second_to_sbuf(second_psum0, 0, GROUP, IMAGES_PER_TILE - GROUP)
+                    second_to_sbuf(second_psum2, 2, GROUP, IMAGES_PER_TILE - GROUP)
+                    quantise_tokens(1)
+                    bias2_psum = psum.tile([P, E_TILES], F32, tag="bank")
+                    for n in range(E_TILES):
+                        nc.tensor.matmul(
+                            bias2_psum[:, n : n + 1],
+                            lhsT=bias2_row[:, n * P : (n + 1) * P],
+                            rhs=unit[:],
+                            start=True,
+                            stop=True,
+                        )
+                    nc.scalar.copy(out=bias2[:], in_=bias2_psum[:])
+                multiplied.append((k, multiply_group(halves)))
+                if k % 2 == 1:
+                    multiplied.append(
+                        (VECTOR_GROUPS + k // 2, multiply_group(gpsimd_halves[k - 1 : k + 1]))
                     )
-            ready = [(k, [quantise_half(h_grouped) for h_grouped in from_vector])]
-            gpsimd_halves.append(quantise_half(from_gpsimd))
-            if k % 2 == 1:
-                ready.append((VECTOR_GROUPS + k // 2, gpsimd_halves[k - 1 : k + 1]))
-            if k == 0:
-                second_to_sbuf(second_psum1, 1)
-            copy = nc.vector.tensor_copy if k == VECTOR_GROUPS - 1 else nc.scalar.copy
-            for g, halves in ready:
-                out_t = multiply_group(halves)
-                if previous is not None:
-                    store_group(previous[0], previous[1], copy)
-                previous = (g, out_t)
-        store_group(previous[0], previous[1], nc.vector.tensor_copy)
+                if k == 0:
+                    first_psum[1] = psum_keep.tile([P, PACK, P], F32, name="first_psum1", tag="shared")
+                    second_psum1 = psum.tile([P, PACK, P], F32, tag="bank")
+                    for t in range(PACK):
+                        first_matmul(second_psum1, 1, 1, t)
+                        first_matmul(first_psum[1], 0, 1, t)
+                if k == 1:
+                    second_to_sbuf(second_psum1, 1, 0, IMAGES_PER_TILE)

@@ -16,7 +16,6 @@ IMAGES = 24
 TOKENS = 16
 PAIRS = TOKENS // 2
 E = 512
-E_TILES = E // P
 PACK = 4
 K_PASS = P * PACK
 TOKEN_TILES = IMAGES * TOKENS // P
@@ -54,22 +53,24 @@ def tile_simplemodel_pb_kernel(tc, tok, corr_w, corr_b, cross_w, cross_b, out):
                 out=w1_sb[:, t * 2 * E : (t + 1) * 2 * E], in_=w1_dram[t]
             )
         nc.sync.dma_start(out=tok_view[:, 1:], in_=tok_dram[:, 1:])
-        w2_sb = keep.tile([P, E_TILES * 2 * E], BF16)
-        w2_dram = cross_w.rearrange("(n p) k -> p n k", p=P)
+        w2_sb = keep.tile([P, PACK * 2 * E], BF16)
+        w2_dram = cross_w.rearrange("(p t) k -> p t k", t=PACK)
         for half in range(2):
             nc.sync.dma_start(
-                out=w2_sb[:, half * 4 * E : (half + 1) * 4 * E].rearrange("p (n k) -> p n k", n=2),
+                out=w2_sb[:, half * 4 * E : (half + 1) * 4 * E].rearrange("p (t k) -> p t k", t=2),
                 in_=w2_dram[:, 2 * half : 2 * half + 2, :],
             )
         bias2_row = keep.tile([P, E], BF16)
         nc.sync.dma_start(out=bias2_row[:], in_=cross_b.partition_broadcast(P))
         bias1 = keep.tile([P, PACK], BF16)
         nc.scalar.dma_start(out=bias1[:], in_=corr_b.rearrange("(p t) -> p t", t=PACK))
+        bias2 = keep.tile([P, PACK], BF16)
+        nc.scalar.dma_start(out=bias2[:], in_=cross_b.rearrange("(p t) -> p t", t=PACK))
 
         ident = keep.tile([P, P], F32)
         make_identity(nc, ident[:])
-        unit = keep.tile([P, 1], BF16)
-        nc.scalar.activation(out=unit[:], in_=ident[:, 0:1], func=IDENTITY)
+        table_loaded = keep.tile([P, 1], F32)
+        nc.scalar.activation(out=table_loaded[:], in_=ident[:, 0:1], func=IDENTITY)
 
         tok_grouped = keep.tile([P, TOKEN_TILES * P * PACK], BF16, align_bytes=64)
         tok_codes = keep.tile([P, TOKEN_TILES * P], U32, align_bytes=64)
@@ -80,7 +81,6 @@ def tile_simplemodel_pb_kernel(tc, tok, corr_w, corr_b, cross_w, cross_b, out):
         w2_grouped = keep.tile([P, 2 * E * PACK], BF16, align_bytes=64)
         w2_codes = keep.tile([P, 2 * E], U32, align_bytes=64)
         w2_scales = keep.tile([P, 2 * E], U8, align_bytes=64)
-        bias2 = keep.tile([P, E_TILES], F32)
         second = keep.tile([P, IMAGES, 2, PAIRS, PACK], F32)
         first_sbuf = keep.tile([P, P, PACK], F32)
 
@@ -132,12 +132,12 @@ def tile_simplemodel_pb_kernel(tc, tok, corr_w, corr_b, cross_w, cross_b, out):
                 in_=w1_grouped[:, start * PACK : stop * PACK],
             )
 
-        def transpose_cross_w(n):
-            bank = transpose_words(w2_words, n * E, 2)
+        def transpose_cross_w(t):
+            bank = transpose_words(w2_words, t * E, 2)
             nc.scalar.copy(
                 out=w2_grouped[:]
                 .bitcast(F32)
-                .rearrange("q (c n r u) -> q n c r u", c=2, n=E_TILES, u=2)[:, n],
+                .rearrange("q (c t r u) -> q t c r u", c=2, t=PACK, u=2)[:, t],
                 in_=bank[:].rearrange("q (c u) r -> q c r u", u=2),
             )
 
@@ -207,8 +207,8 @@ def tile_simplemodel_pb_kernel(tc, tok, corr_w, corr_b, cross_w, cross_b, out):
             first_matmul(first_psum2, 0, 2, t)
         nc.scalar.copy(out=first_sbuf[:], in_=first_psum2[:].rearrange("q t r -> q r t"))
         second_to_sbuf(second_psum2, 2, 0, GROUP)
-        for n in range(1, E_TILES):
-            transpose_cross_w(n)
+        for t in range(1, PACK):
+            transpose_cross_w(t)
 
         full = [P, GROUP, TOKENS, PAIRS, PACK]
 
@@ -247,14 +247,14 @@ def tile_simplemodel_pb_kernel(tc, tok, corr_w, corr_b, cross_w, cross_b, out):
             return h_codes, h_scales
 
         def multiply_group(halves):
-            out_t = out_pool.tile([P, E_TILES, GROUP_ROWS], F32)
-            for pair in range(E_TILES // 2):
+            out_t = out_pool.tile([P, PACK, GROUP_ROWS], F32)
+            for pair in range(PACK // 2):
                 acc = psum.tile([P, 2, GROUP_ROWS], F32, tag="bank")
                 for s in range(2):
-                    n = 2 * pair + s
+                    t = 2 * pair + s
                     for c in range(2):
                         h_codes, h_scales = halves[c]
-                        w_cols = slice(c * E + n * P, c * E + (n + 1) * P)
+                        w_cols = slice(c * E + t * P, c * E + (t + 1) * P)
                         nc.tensor.matmul_mx(
                             out=acc[:, s, :],
                             lhsT=w2_codes[:, w_cols].bitcast(FP8X4),
@@ -265,34 +265,40 @@ def tile_simplemodel_pb_kernel(tc, tok, corr_w, corr_b, cross_w, cross_b, out):
                             stop=(c == 1),
                         )
                 for s in range(2):
-                    n = 2 * pair + s
+                    t = 2 * pair + s
                     nc.scalar.activation(
-                        out=out_t[:, n, :],
+                        out=out_t[:, t, :],
                         in_=acc[:, s, :],
                         func=IDENTITY,
-                        bias=bias2[:, n : n + 1],
+                        bias=bias2[:, t : t + 1],
                         scale=1.0,
                     )
             return out_t
 
-        def store_group(g, out_t):
+        def store_image(queue, g, b, result):
+            row0 = (g * GROUP + b) * P
+            queue.dma_start(out=out_rows[row0 : row0 + P, :], in_=result[:])
+
+        def store_group(queue, g, out_t):
             for b in range(GROUP):
-                back = psum.tile([P, E_TILES, P], F32, tag="bank")
-                for n in range(E_TILES):
-                    nc.tensor.transpose(back[:, n, :], out_t[:, n, b * P : (b + 1) * P], ident[:])
+                back = psum.tile([P, PACK, P], F32, tag="bank")
+                for t in range(PACK):
+                    nc.tensor.transpose(back[:, t, :], out_t[:, t, b * P : (b + 1) * P], ident[:])
                 result = out_pool.tile([P, E], F32)
-                nc.scalar.copy(out=result[:], in_=back[:].rearrange("r n e -> r (n e)"))
-                row0 = (g * GROUP + b) * P
-                nc.sync.dma_start(out=out_rows[row0 : row0 + P, :], in_=result[:])
+                nc.scalar.copy(
+                    out=result[:].rearrange("i (r t) -> i r t", t=PACK),
+                    in_=back[:].rearrange("i t r -> i r t"),
+                )
+                store_image(queue, g, b, result)
 
         def multiply_direct(halves):
             banks = []
             for b in range(GROUP):
-                acc = psum.tile([P, E], F32, tag="bank")
+                acc = psum.tile([P, PACK, P], F32, tag="bank")
                 for c in range(2):
                     h_codes, h_scales = halves[c]
                     nc.tensor.matmul_mx(
-                        out=acc[:],
+                        out=acc[:].rearrange("i t r -> i (t r)"),
                         lhsT=h_codes[:, b * P : (b + 1) * P].bitcast(FP8X4),
                         lhsT_scale=h_scales[:, b * P : (b + 1) * P],
                         rhs=w2_codes[:, c * E : (c + 1) * E].bitcast(FP8X4),
@@ -306,9 +312,13 @@ def tile_simplemodel_pb_kernel(tc, tok, corr_w, corr_b, cross_w, cross_b, out):
         def store_direct(g, banks):
             for b in range(GROUP):
                 result = out_pool.tile([P, E], F32, tag="direct")
-                nc.vector.tensor_tensor(out=result[:], in0=banks[b][:], in1=bias2_row[:], op=ADD)
-                row0 = (g * GROUP + b) * P
-                nc.sync.dma_start(out=out_rows[row0 : row0 + P, :], in_=result[:])
+                nc.vector.tensor_tensor(
+                    out=result[:].rearrange("i (r t) -> i r t", t=PACK),
+                    in0=banks[b][:].rearrange("i t r -> i r t"),
+                    in1=bias2_row[:].rearrange("i (r t) -> i r t", t=PACK),
+                    op=ADD,
+                )
+                store_image(nc.sync, g, b, result)
 
         gpsimd_halves = []
         multiplied = []
@@ -318,7 +328,7 @@ def tile_simplemodel_pb_kernel(tc, tok, corr_w, corr_b, cross_w, cross_b, out):
             from_vector = [add_half(k, c) for c in range(2)]
             if not last_round:
                 for g, out_t in multiplied:
-                    store_group(g, out_t)
+                    store_group(nc.sync, g, out_t)
                 multiplied = []
             if k == 0:
                 quantise_cross_w(0)
@@ -330,7 +340,7 @@ def tile_simplemodel_pb_kernel(tc, tok, corr_w, corr_b, cross_w, cross_b, out):
                     (k, multiply_direct(halves)),
                 ]
                 for g, out_t in multiplied:
-                    store_group(g, out_t)
+                    store_group(nc.scalar, g, out_t)
                 for g, banks in direct:
                     store_direct(g, banks)
             else:
@@ -342,16 +352,6 @@ def tile_simplemodel_pb_kernel(tc, tok, corr_w, corr_b, cross_w, cross_b, out):
                     second_to_sbuf(second_psum0, 0, GROUP, IMAGES_PER_TILE - GROUP)
                     second_to_sbuf(second_psum2, 2, GROUP, IMAGES_PER_TILE - GROUP)
                     quantise_tokens(1)
-                    bias2_psum = psum.tile([P, E_TILES], F32, tag="bank")
-                    for n in range(E_TILES):
-                        nc.tensor.matmul(
-                            bias2_psum[:, n : n + 1],
-                            lhsT=bias2_row[:, n * P : (n + 1) * P],
-                            rhs=unit[:],
-                            start=True,
-                            stop=True,
-                        )
-                    nc.scalar.copy(out=bias2[:], in_=bias2_psum[:])
                 multiplied.append((k, multiply_group(halves)))
                 if k % 2 == 1:
                     multiplied.append(

@@ -20,10 +20,10 @@ PACK = 4
 K_PASS = P * PACK
 TOKEN_TILES = IMAGES * TOKENS // P
 IMAGES_PER_TILE = P // TOKENS
-GROUP = 2
-GROUP_ROWS = GROUP * P
-VECTOR_TILES = 2
-VECTOR_GROUPS = VECTOR_TILES * IMAGES_PER_TILE // GROUP
+ROUND = 4
+ROUNDS = IMAGES // ROUND
+VECTOR_ROUND = 3
+VECTOR_IMAGES = VECTOR_ROUND * ROUNDS
 
 FLOPS = 2 * IMAGES * TOKENS * TOKENS * 2 * E * E + 2 * IMAGES * TOKENS * PAIRS * 2 * E * E
 
@@ -36,8 +36,8 @@ def tile_simplemodel_pb_kernel(tc, tok, corr_w, corr_b, cross_w, cross_b, out):
     with ExitStack() as stack:
         stack.enter_context(tc.manual_schedule())
         keep = stack.enter_context(tc.tile_pool(name="keep", bufs=1))
-        h_pool = stack.enter_context(tc.tile_pool(name="h", bufs=4))
-        code_pool = stack.enter_context(tc.tile_pool(name="codes", bufs=6))
+        h_pool = stack.enter_context(tc.tile_pool(name="h", bufs=6))
+        code_pool = stack.enter_context(tc.tile_pool(name="codes", bufs=4))
         out_pool = stack.enter_context(tc.tile_pool(name="o", bufs=4))
         psum_keep = stack.enter_context(tc.psum_pool(name="psum_keep", bufs=1))
         psum = stack.enter_context(tc.psum_pool(name="psum", bufs=6))
@@ -176,8 +176,8 @@ def tile_simplemodel_pb_kernel(tc, tok, corr_w, corr_b, cross_w, cross_b, out):
                 )
 
         first_psum = {}
-        first_psum[0] = psum_keep.tile([P, PACK, P], F32, name="first_psum0")
-        second_psum0 = psum_keep.tile([P, PACK, P], F32, name="second_psum0", tag="shared")
+        first_psum[0] = psum_keep.tile([P, PACK, P], F32, name="first_psum0", tag="even")
+        second_psum0 = psum_keep.tile([P, PACK, P], F32, name="second_psum0", tag="odd")
         transpose_tokens(0)
         quantise_tokens(0)
         for t in range(3):
@@ -197,7 +197,7 @@ def tile_simplemodel_pb_kernel(tc, tok, corr_w, corr_b, cross_w, cross_b, out):
         quantise_tokens(2)
         first_matmul(second_psum0, 1, 0, 3)
         first_matmul(first_psum[0], 0, 0, 3)
-        second_to_sbuf(second_psum0, 0, 0, GROUP)
+        second_to_sbuf(second_psum0, 0, 0, VECTOR_ROUND)
 
         transpose_cross_w(0)
         second_psum2 = psum.tile([P, PACK, P], F32, tag="bank")
@@ -206,162 +206,153 @@ def tile_simplemodel_pb_kernel(tc, tok, corr_w, corr_b, cross_w, cross_b, out):
             first_matmul(second_psum2, 1, 2, t)
             first_matmul(first_psum2, 0, 2, t)
         nc.scalar.copy(out=first_sbuf[:], in_=first_psum2[:].rearrange("q t r -> q r t"))
-        second_to_sbuf(second_psum2, 2, 0, GROUP)
+        gpsimd_image = VECTOR_IMAGES % IMAGES_PER_TILE
+        second_to_sbuf(second_psum2, 2, gpsimd_image, 1)
         for t in range(1, PACK):
             transpose_cross_w(t)
 
-        full = [P, GROUP, TOKENS, PAIRS, PACK]
-
-        def add_half(g, c):
-            b0 = g * GROUP
-            t0 = (b0 % IMAGES_PER_TILE) * TOKENS
-            if g < VECTOR_GROUPS:
-                engine = nc.vector
-                h_grouped = h_pool.tile([P, GROUP, P * PACK], BF16, align_bytes=64, tag="h_vector")
-                bank = first_psum[b0 // IMAGES_PER_TILE]
-                first = bank[:, :, t0 : t0 + GROUP * TOKENS].rearrange("q t (b i) -> q b i t", b=GROUP)
-            else:
-                engine = nc.gpsimd
-                h_grouped = h_pool.tile(
-                    [P, GROUP, P * PACK], BF16, align_bytes=64, tag="h_gpsimd", bufs=1
-                )
-                first = first_sbuf[:, t0 : t0 + GROUP * TOKENS, :].rearrange(
-                    "q (b i) t -> q b i t", b=GROUP
-                )
+        def add(engine, first, b0, images, c, h_grouped):
+            full = [P, images, TOKENS, PAIRS, PACK]
             engine.tensor_tensor(
-                out=h_grouped[:].rearrange("q b (i m t) -> q b i m t", i=TOKENS, m=PAIRS),
+                out=h_grouped.rearrange("q b (i m t) -> q b i m t", i=TOKENS, m=PAIRS),
                 in0=first.unsqueeze(3).to_broadcast(full),
-                in1=second[:, b0 : b0 + GROUP, c].unsqueeze(2).to_broadcast(full),
+                in1=second[:, b0 : b0 + images, c].unsqueeze(2).to_broadcast(full),
                 op=ADD,
             )
+
+        def add_on_vector(b0, images, c):
+            h_grouped = h_pool.tile([P, 2, P * PACK], BF16, align_bytes=64, tag="h_vector")
+            t0 = (b0 % IMAGES_PER_TILE) * TOKENS
+            bank = first_psum[b0 // IMAGES_PER_TILE]
+            first = bank[:, :, t0 : t0 + images * TOKENS].rearrange("q t (b i) -> q b i t", b=images)
+            add(nc.vector, first, b0, images, c, h_grouped[:, 0:images])
             return h_grouped
 
-        def quantise_half(h_grouped):
-            h_codes = code_pool.tile([P, GROUP_ROWS], U32, align_bytes=64)
-            h_scales = code_pool.tile([P, GROUP_ROWS], U8, align_bytes=64)
-            nc.vector.quantize_mx(
-                out=h_codes[:].bitcast(FP8X4),
-                scales=h_scales[:],
-                in_=h_grouped[:].rearrange("q b x -> q (b x)"),
+        def add_on_gpsimd(b, c):
+            h_grouped = h_pool.tile(
+                [P, 1, P * PACK], BF16, align_bytes=64, name="h_gpsimd%d" % c, bufs=1
             )
-            return h_codes, h_scales
+            t0 = (b % IMAGES_PER_TILE) * TOKENS
+            first = first_sbuf[:, t0 : t0 + TOKENS, :].unsqueeze(1)
+            add(nc.gpsimd, first, b, 1, c, h_grouped[:])
+            return h_grouped
 
-        def multiply_group(halves):
-            out_t = out_pool.tile([P, PACK, GROUP_ROWS], F32)
-            for pair in range(PACK // 2):
-                acc = psum.tile([P, 2, GROUP_ROWS], F32, tag="bank")
-                for s in range(2):
-                    t = 2 * pair + s
-                    for c in range(2):
-                        h_codes, h_scales = halves[c]
-                        w_cols = slice(c * E + t * P, c * E + (t + 1) * P)
-                        nc.tensor.matmul_mx(
-                            out=acc[:, s, :],
-                            lhsT=w2_codes[:, w_cols].bitcast(FP8X4),
-                            lhsT_scale=w2_scales[:, w_cols],
-                            rhs=h_codes[:].bitcast(FP8X4),
-                            rhs_scale=h_scales[:],
-                            start=(c == 0),
-                            stop=(c == 1),
-                        )
-                for s in range(2):
-                    t = 2 * pair + s
-                    nc.scalar.activation(
-                        out=out_t[:, t, :],
-                        in_=acc[:, s, :],
-                        func=IDENTITY,
-                        bias=bias2[:, t : t + 1],
-                        scale=1.0,
+        def quantise(h_grouped, images, codes, scales, slot):
+            cols = slice(slot * P, (slot + images) * P)
+            nc.vector.quantize_mx(
+                out=codes[:, cols].bitcast(FP8X4),
+                scales=scales[:, cols],
+                in_=h_grouped[:, 0:images].rearrange("q b x -> q (b x)"),
+            )
+
+        def multiply_round(codes, scales):
+            out_t = out_pool.tile([P, PACK, ROUND * P], F32, bufs=2)
+            for t in range(PACK):
+                acc = psum.tile([P, ROUND * P], F32, tag="bank")
+                for c in range(2):
+                    w_cols = slice(c * E + t * P, c * E + (t + 1) * P)
+                    nc.tensor.matmul_mx(
+                        out=acc[:],
+                        lhsT=w2_codes[:, w_cols].bitcast(FP8X4),
+                        lhsT_scale=w2_scales[:, w_cols],
+                        rhs=codes[c][:].bitcast(FP8X4),
+                        rhs_scale=scales[c][:],
+                        start=(c == 0),
+                        stop=(c == 1),
                     )
+                nc.scalar.activation(
+                    out=out_t[:, t, :],
+                    in_=acc[:],
+                    func=IDENTITY,
+                    bias=bias2[:, t : t + 1],
+                    scale=1.0,
+                )
             return out_t
 
-        def store_image(queue, g, b, result):
-            row0 = (g * GROUP + b) * P
-            queue.dma_start(out=out_rows[row0 : row0 + P, :], in_=result[:])
+        def store_image(queue, b, result):
+            queue.dma_start(out=out_rows[b * P : (b + 1) * P, :], in_=result[:])
 
-        def store_group(queue, g, out_t):
-            for b in range(GROUP):
+        def store_round(queue, images, out_t):
+            for slot, b in enumerate(images):
                 back = psum.tile([P, PACK, P], F32, tag="bank")
                 for t in range(PACK):
-                    nc.tensor.transpose(back[:, t, :], out_t[:, t, b * P : (b + 1) * P], ident[:])
+                    nc.tensor.transpose(back[:, t, :], out_t[:, t, slot * P : (slot + 1) * P], ident[:])
                 result = out_pool.tile([P, E], F32)
                 nc.scalar.copy(
                     out=result[:].rearrange("i (r t) -> i r t", t=PACK),
                     in_=back[:].rearrange("i t r -> i r t"),
                 )
-                store_image(queue, g, b, result)
+                store_image(queue, b, result)
 
-        def multiply_direct(halves):
-            banks = []
-            for b in range(GROUP):
-                acc = psum.tile([P, PACK, P], F32, tag="bank")
-                for c in range(2):
-                    h_codes, h_scales = halves[c]
-                    nc.tensor.matmul_mx(
-                        out=acc[:].rearrange("i t r -> i (t r)"),
-                        lhsT=h_codes[:, b * P : (b + 1) * P].bitcast(FP8X4),
-                        lhsT_scale=h_scales[:, b * P : (b + 1) * P],
-                        rhs=w2_codes[:, c * E : (c + 1) * E].bitcast(FP8X4),
-                        rhs_scale=w2_scales[:, c * E : (c + 1) * E],
-                        start=(c == 0),
-                        stop=(c == 1),
-                    )
-                banks.append(acc)
-            return banks
-
-        def store_direct(g, banks):
-            for b in range(GROUP):
-                result = out_pool.tile([P, E], F32, tag="direct")
-                nc.vector.tensor_tensor(
-                    out=result[:].rearrange("i (r t) -> i r t", t=PACK),
-                    in0=banks[b][:].rearrange("i t r -> i r t"),
-                    in1=bias2_row[:].rearrange("i (r t) -> i r t", t=PACK),
-                    op=ADD,
+        def multiply_direct(codes, scales, slot):
+            rows = slice(slot * P, (slot + 1) * P)
+            acc = psum.tile([P, PACK, P], F32, tag="bank")
+            for c in range(2):
+                nc.tensor.matmul_mx(
+                    out=acc[:].rearrange("i t r -> i (t r)"),
+                    lhsT=codes[c][:, rows].bitcast(FP8X4),
+                    lhsT_scale=scales[c][:, rows],
+                    rhs=w2_codes[:, c * E : (c + 1) * E].bitcast(FP8X4),
+                    rhs_scale=w2_scales[:, c * E : (c + 1) * E],
+                    start=(c == 0),
+                    stop=(c == 1),
                 )
-                store_image(nc.sync, g, b, result)
+            return acc
 
-        gpsimd_halves = []
-        multiplied = []
-        for k in range(VECTOR_GROUPS):
-            last_round = k == VECTOR_GROUPS - 1
-            from_gpsimd = add_half(VECTOR_GROUPS + k // 2, k % 2)
-            from_vector = [add_half(k, c) for c in range(2)]
-            if not last_round:
-                for g, out_t in multiplied:
-                    store_group(nc.sync, g, out_t)
-                multiplied = []
+        def store_direct(b, acc):
+            result = out_pool.tile([P, E], F32, tag="direct")
+            nc.vector.tensor_tensor(
+                out=result[:].rearrange("i (r t) -> i r t", t=PACK),
+                in0=acc[:].rearrange("i t r -> i r t"),
+                in1=bias2_row[:].rearrange("i (r t) -> i r t", t=PACK),
+                op=ADD,
+            )
+            store_image(nc.sync, b, result)
+
+        multiplied = None
+        for k in range(ROUNDS):
+            last_round = k == ROUNDS - 1
+            codes = [code_pool.tile([P, ROUND * P], U32, align_bytes=64, name="h_codes") for c in range(2)]
+            scales = [code_pool.tile([P, ROUND * P], U8, align_bytes=64, name="h_scales") for c in range(2)]
+            b0 = k * VECTOR_ROUND
+            images = [b0 + i for i in range(VECTOR_ROUND)] + [VECTOR_IMAGES + k]
+            from_gpsimd = [add_on_gpsimd(VECTOR_IMAGES + k, c) for c in range(2)]
+            if b0 // IMAGES_PER_TILE == (b0 + 1) // IMAGES_PER_TILE:
+                parts = [(0, 2), (2, 1)]
+            else:
+                parts = [(0, 1), (1, 2)]
+            from_vector = []
+            for slot, count in parts:
+                for c in range(2):
+                    from_vector.append((add_on_vector(b0 + slot, count, c), count, c, slot))
+            if multiplied is not None:
+                store_round(nc.sync, *multiplied)
             if k == 0:
                 quantise_cross_w(0)
+                quantise_cross_w(1)
+            for h_grouped, count, c, slot in from_vector:
+                quantise(h_grouped, count, codes[c], scales[c], slot)
+            for c in range(2):
+                quantise(from_gpsimd[c], 1, codes[c], scales[c], VECTOR_ROUND)
             if last_round:
-                gpsimd_halves.append(quantise_half(from_gpsimd))
-                halves = [quantise_half(h_grouped) for h_grouped in from_vector]
-                direct = [
-                    (VECTOR_GROUPS + k // 2, multiply_direct(gpsimd_halves[k - 1 : k + 1])),
-                    (k, multiply_direct(halves)),
-                ]
-                for g, out_t in multiplied:
-                    store_group(nc.scalar, g, out_t)
-                for g, banks in direct:
-                    store_direct(g, banks)
+                banks = [multiply_direct(codes, scales, slot) for slot in range(ROUND)]
+                for b, acc in zip(images, banks):
+                    store_direct(b, acc)
             else:
-                halves = [quantise_half(h_grouped) for h_grouped in from_vector]
-                if k == 0:
-                    quantise_cross_w(1)
-                gpsimd_halves.append(quantise_half(from_gpsimd))
-                if k == 0:
-                    second_to_sbuf(second_psum0, 0, GROUP, IMAGES_PER_TILE - GROUP)
-                    second_to_sbuf(second_psum2, 2, GROUP, IMAGES_PER_TILE - GROUP)
-                    quantise_tokens(1)
-                multiplied.append((k, multiply_group(halves)))
-                if k % 2 == 1:
-                    multiplied.append(
-                        (VECTOR_GROUPS + k // 2, multiply_group(gpsimd_halves[k - 1 : k + 1]))
-                    )
-                if k == 0:
-                    first_psum[1] = psum_keep.tile([P, PACK, P], F32, name="first_psum1", tag="shared")
-                    second_psum1 = psum.tile([P, PACK, P], F32, tag="bank")
-                    for t in range(PACK):
-                        first_matmul(second_psum1, 1, 1, t)
-                        first_matmul(first_psum[1], 0, 1, t)
-                if k == 1:
-                    second_to_sbuf(second_psum1, 1, 0, IMAGES_PER_TILE)
+                multiplied = (images, multiply_round(codes, scales))
+            if k == 0:
+                second_to_sbuf(second_psum0, 0, VECTOR_ROUND, IMAGES_PER_TILE - VECTOR_ROUND)
+                second_to_sbuf(second_psum2, 2, 0, gpsimd_image)
+                second_to_sbuf(second_psum2, 2, gpsimd_image + 1, IMAGES_PER_TILE - gpsimd_image - 1)
+                quantise_tokens(1)
+                first_psum[1] = psum_keep.tile([P, PACK, P], F32, name="first_psum1", tag="odd")
+                second_psum1 = psum.tile([P, PACK, P], F32, tag="bank")
+                for t in range(PACK):
+                    first_matmul(second_psum1, 1, 1, t)
+                    first_matmul(first_psum[1], 0, 1, t)
+            if k == 1:
+                second_to_sbuf(second_psum1, 1, 0, IMAGES_PER_TILE)
+            if k == 3:
+                first_psum[2] = psum_keep.tile([P, PACK, P], F32, name="first_psum2v", tag="even")
+                for t in range(PACK):
+                    first_matmul(first_psum[2], 0, 2, t)

@@ -21,9 +21,10 @@ K_PASS = P * PACK
 TOKEN_TILES = IMAGES * TOKENS // P
 IMAGES_PER_TILE = P // TOKENS
 ROUND = 4
-ROUNDS = IMAGES // ROUND
-VECTOR_ROUND = 3
-VECTOR_IMAGES = VECTOR_ROUND * ROUNDS
+VECTOR_ROUNDS = [2, 3, 3, 3, 3, 3, 1]
+GPSIMD_ROUNDS = [0, 1, 1, 1, 1, 1, 1]
+ROUNDS = len(VECTOR_ROUNDS)
+VECTOR_IMAGES = sum(VECTOR_ROUNDS)
 
 FLOPS = 2 * IMAGES * TOKENS * TOKENS * 2 * E * E + 2 * IMAGES * TOKENS * PAIRS * 2 * E * E
 
@@ -36,9 +37,9 @@ def tile_simplemodel_pb_kernel(tc, tok, corr_w, corr_b, cross_w, cross_b, out):
     with ExitStack() as stack:
         stack.enter_context(tc.manual_schedule())
         keep = stack.enter_context(tc.tile_pool(name="keep", bufs=1))
-        h_pool = stack.enter_context(tc.tile_pool(name="h", bufs=6))
+        h_pool = stack.enter_context(tc.tile_pool(name="h", bufs=1))
         code_pool = stack.enter_context(tc.tile_pool(name="codes", bufs=4))
-        out_pool = stack.enter_context(tc.tile_pool(name="o", bufs=4))
+        out_pool = stack.enter_context(tc.tile_pool(name="o", bufs=6))
         psum_keep = stack.enter_context(tc.psum_pool(name="psum_keep", bufs=1))
         psum = stack.enter_context(tc.psum_pool(name="psum", bufs=6))
 
@@ -195,21 +196,19 @@ def tile_simplemodel_pb_kernel(tc, tok, corr_w, corr_b, cross_w, cross_b, out):
         transpose_tokens(2)
         transpose_tokens(1)
         quantise_tokens(2)
+        quantise_tokens(1)
         first_matmul(second_psum0, 1, 0, 3)
         first_matmul(first_psum[0], 0, 0, 3)
-        second_to_sbuf(second_psum0, 0, 0, VECTOR_ROUND)
+        second_to_sbuf(second_psum0, 0, 0, VECTOR_ROUNDS[0])
+        for t in range(PACK):
+            transpose_cross_w(t)
 
-        transpose_cross_w(0)
         second_psum2 = psum.tile([P, PACK, P], F32, tag="bank")
         first_psum2 = psum.tile([P, PACK, P], F32, tag="bank")
         for t in range(PACK):
             first_matmul(second_psum2, 1, 2, t)
             first_matmul(first_psum2, 0, 2, t)
         nc.scalar.copy(out=first_sbuf[:], in_=first_psum2[:].rearrange("q t r -> q r t"))
-        gpsimd_image = VECTOR_IMAGES % IMAGES_PER_TILE
-        second_to_sbuf(second_psum2, 2, gpsimd_image, 1)
-        for t in range(1, PACK):
-            transpose_cross_w(t)
 
         def add(engine, first, b0, images, c, h_grouped):
             full = [P, images, TOKENS, PAIRS, PACK]
@@ -220,59 +219,48 @@ def tile_simplemodel_pb_kernel(tc, tok, corr_w, corr_b, cross_w, cross_b, out):
                 op=ADD,
             )
 
-        def add_on_vector(b0, images, c):
-            h_grouped = h_pool.tile([P, 2, P * PACK], BF16, align_bytes=64, tag="h_vector")
+        def add_on_vector(b0, images, c, h_grouped):
             t0 = (b0 % IMAGES_PER_TILE) * TOKENS
             bank = first_psum[b0 // IMAGES_PER_TILE]
             first = bank[:, :, t0 : t0 + images * TOKENS].rearrange("q t (b i) -> q b i t", b=images)
-            add(nc.vector, first, b0, images, c, h_grouped[:, 0:images])
-            return h_grouped
+            add(nc.vector, first, b0, images, c, h_grouped)
 
-        def add_on_gpsimd(b, c):
-            h_grouped = h_pool.tile(
-                [P, 1, P * PACK], BF16, align_bytes=64, name="h_gpsimd%d" % c, bufs=1
-            )
+        def add_on_gpsimd(b, c, h_grouped):
             t0 = (b % IMAGES_PER_TILE) * TOKENS
             first = first_sbuf[:, t0 : t0 + TOKENS, :].unsqueeze(1)
-            add(nc.gpsimd, first, b, 1, c, h_grouped[:])
-            return h_grouped
+            add(nc.gpsimd, first, b, 1, c, h_grouped)
 
-        def quantise(h_grouped, images, codes, scales, slot):
-            cols = slice(slot * P, (slot + images) * P)
-            nc.vector.quantize_mx(
-                out=codes[:, cols].bitcast(FP8X4),
-                scales=scales[:, cols],
-                in_=h_grouped[:, 0:images].rearrange("q b x -> q (b x)"),
-            )
-
-        def multiply_round(codes, scales):
+        def multiply(codes, scales, count):
+            rows = slice(0, count * P)
             out_t = out_pool.tile([P, PACK, ROUND * P], F32, bufs=2)
-            for t in range(PACK):
-                acc = psum.tile([P, ROUND * P], F32, tag="bank")
-                for c in range(2):
-                    w_cols = slice(c * E + t * P, c * E + (t + 1) * P)
-                    nc.tensor.matmul_mx(
-                        out=acc[:],
-                        lhsT=w2_codes[:, w_cols].bitcast(FP8X4),
-                        lhsT_scale=w2_scales[:, w_cols],
-                        rhs=codes[c][:].bitcast(FP8X4),
-                        rhs_scale=scales[c][:],
-                        start=(c == 0),
-                        stop=(c == 1),
+            for t0 in range(0, PACK, ROUND // count):
+                acc = psum.tile([P, ROUND // count, count * P], F32, tag="bank")
+                for s in range(ROUND // count):
+                    for c in range(2):
+                        w_cols = slice(c * E + (t0 + s) * P, c * E + (t0 + s + 1) * P)
+                        nc.tensor.matmul_mx(
+                            out=acc[:, s, :],
+                            lhsT=w2_codes[:, w_cols].bitcast(FP8X4),
+                            lhsT_scale=w2_scales[:, w_cols],
+                            rhs=codes[c][:, rows].bitcast(FP8X4),
+                            rhs_scale=scales[c][:, rows],
+                            start=(c == 0),
+                            stop=(c == 1),
+                        )
+                for s in range(ROUND // count):
+                    nc.scalar.activation(
+                        out=out_t[:, t0 + s, rows],
+                        in_=acc[:, s, :],
+                        func=IDENTITY,
+                        bias=bias2[:, t0 + s : t0 + s + 1],
+                        scale=1.0,
                     )
-                nc.scalar.activation(
-                    out=out_t[:, t, :],
-                    in_=acc[:],
-                    func=IDENTITY,
-                    bias=bias2[:, t : t + 1],
-                    scale=1.0,
-                )
             return out_t
 
         def store_image(queue, b, result):
             queue.dma_start(out=out_rows[b * P : (b + 1) * P, :], in_=result[:])
 
-        def store_round(queue, images, out_t):
+        def turn_back(queue, images, out_t):
             for slot, b in enumerate(images):
                 back = psum.tile([P, PACK, P], F32, tag="bank")
                 for t in range(PACK):
@@ -310,41 +298,58 @@ def tile_simplemodel_pb_kernel(tc, tok, corr_w, corr_b, cross_w, cross_b, out):
             store_image(nc.sync, b, result)
 
         multiplied = None
+        direct = []
+        v0, g0 = 0, VECTOR_IMAGES
         for k in range(ROUNDS):
-            last_round = k == ROUNDS - 1
-            codes = [code_pool.tile([P, ROUND * P], U32, align_bytes=64, name="h_codes") for c in range(2)]
-            scales = [code_pool.tile([P, ROUND * P], U8, align_bytes=64, name="h_scales") for c in range(2)]
-            b0 = k * VECTOR_ROUND
-            images = [b0 + i for i in range(VECTOR_ROUND)] + [VECTOR_IMAGES + k]
-            from_gpsimd = [add_on_gpsimd(VECTOR_IMAGES + k, c) for c in range(2)]
-            if b0 // IMAGES_PER_TILE == (b0 + 1) // IMAGES_PER_TILE:
-                parts = [(0, 2), (2, 1)]
-            else:
-                parts = [(0, 1), (1, 2)]
-            from_vector = []
-            for slot, count in parts:
-                for c in range(2):
-                    from_vector.append((add_on_vector(b0 + slot, count, c), count, c, slot))
-            if multiplied is not None:
-                store_round(nc.sync, *multiplied)
+            vector_images = [v0 + i for i in range(VECTOR_ROUNDS[k])]
+            gpsimd_images = [g0 + i for i in range(GPSIMD_ROUNDS[k])]
+            v0 += VECTOR_ROUNDS[k]
+            g0 += GPSIMD_ROUNDS[k]
+            images = vector_images + gpsimd_images
+            h_tiles = []
+            for c in range(2):
+                h_grouped = h_pool.tile([P, ROUND, P * PACK], BF16, align_bytes=64, name="h%d" % c)
+                h_tiles.append(h_grouped)
+                for slot, b in enumerate(images):
+                    if b in gpsimd_images:
+                        add_on_gpsimd(b, c, h_grouped[:, slot : slot + 1])
+                slot = 0
+                while slot < len(vector_images):
+                    b = vector_images[slot]
+                    count = min(len(vector_images) - slot, IMAGES_PER_TILE - b % IMAGES_PER_TILE)
+                    add_on_vector(b, count, c, h_grouped[:, slot : slot + count])
+                    slot += count
+            for b, acc in direct:
+                store_direct(b, acc)
+            direct = []
             if k == 0:
                 quantise_cross_w(0)
-                quantise_cross_w(1)
-            for h_grouped, count, c, slot in from_vector:
-                quantise(h_grouped, count, codes[c], scales[c], slot)
+            codes, scales = [], []
             for c in range(2):
-                quantise(from_gpsimd[c], 1, codes[c], scales[c], VECTOR_ROUND)
-            if last_round:
-                banks = [multiply_direct(codes, scales, slot) for slot in range(ROUND)]
-                for b, acc in zip(images, banks):
-                    store_direct(b, acc)
-            else:
-                multiplied = (images, multiply_round(codes, scales))
+                h_codes = code_pool.tile([P, ROUND * P], U32, align_bytes=64)
+                h_scales = code_pool.tile([P, ROUND * P], U8, align_bytes=64)
+                nc.vector.quantize_mx(
+                    out=h_codes[:, 0 : len(images) * P].bitcast(FP8X4),
+                    scales=h_scales[:, 0 : len(images) * P],
+                    in_=h_tiles[c][:, 0 : len(images)].rearrange("q b x -> q (b x)"),
+                )
+                codes.append(h_codes)
+                scales.append(h_scales)
             if k == 0:
-                second_to_sbuf(second_psum0, 0, VECTOR_ROUND, IMAGES_PER_TILE - VECTOR_ROUND)
-                second_to_sbuf(second_psum2, 2, 0, gpsimd_image)
-                second_to_sbuf(second_psum2, 2, gpsimd_image + 1, IMAGES_PER_TILE - gpsimd_image - 1)
-                quantise_tokens(1)
+                quantise_cross_w(1)
+                second_to_sbuf(second_psum2, 2, 0, IMAGES_PER_TILE)
+                second_to_sbuf(
+                    second_psum0, 0, VECTOR_ROUNDS[0], IMAGES_PER_TILE - VECTOR_ROUNDS[0]
+                )
+            turned = len(images) if k < ROUNDS - 2 else 0
+            previous, multiplied = multiplied, None
+            if turned > 0:
+                multiplied = (images[0:turned], multiply(codes, scales, turned))
+            for slot in range(turned, len(images)):
+                direct.append((images[slot], multiply_direct(codes, scales, slot)))
+            if previous is not None:
+                turn_back(nc.scalar if k == ROUNDS - 1 else nc.sync, *previous)
+            if k == 0:
                 first_psum[1] = psum_keep.tile([P, PACK, P], F32, name="first_psum1", tag="odd")
                 second_psum1 = psum.tile([P, PACK, P], F32, tag="bank")
                 for t in range(PACK):
@@ -356,3 +361,5 @@ def tile_simplemodel_pb_kernel(tc, tok, corr_w, corr_b, cross_w, cross_b, out):
                 first_psum[2] = psum_keep.tile([P, PACK, P], F32, name="first_psum2v", tag="even")
                 for t in range(PACK):
                     first_matmul(first_psum[2], 0, 2, t)
+        for b, acc in direct:
+            store_direct(b, acc)

@@ -68,6 +68,8 @@ def tile_simplemodel_pb_kernel(tc, tok, corr_w, corr_b, cross_w, cross_b, out):
         bias2 = keep.tile([P, PACK], BF16)
         nc.scalar.dma_start(out=bias2[:], in_=cross_b.rearrange("(p t) -> p t", t=PACK))
 
+        zeros = keep.tile([P, P], BF16)
+        nc.vector.memset(zeros[:], 0.0)
         ident = keep.tile([P, P], F32)
         make_identity(nc, ident[:])
         table_loaded = keep.tile([P, 1], F32)
@@ -176,12 +178,36 @@ def tile_simplemodel_pb_kernel(tc, tok, corr_w, corr_b, cross_w, cross_b, out):
                     op=ADD,
                 )
 
+        def second_on_scalar(product, n):
+            out_view = second[:, n * IMAGES_PER_TILE : (n + 1) * IMAGES_PER_TILE]
+            for t in range(PACK):
+                nc.scalar.activation(
+                    out=out_view[:, :, :, :, t],
+                    in_=product[:, t, :].rearrange("q (b m c) -> q b c m", m=PAIRS, c=2),
+                    func=IDENTITY,
+                    bias=bias1[:, t : t + 1],
+                    scale=1.0,
+                )
+
         first_psum = {}
         first_psum[0] = psum_keep.tile([P, PACK, P], F32, name="first_psum0", tag="even")
         second_psum0 = psum_keep.tile([P, PACK, P], F32, name="second_psum0", tag="odd")
+
+        def keep_clock(passes):
+            for n in range(passes):
+                nc.tensor.matmul(
+                    first_psum[0][:].rearrange("q t r -> q (t r)"),
+                    lhsT=zeros[:],
+                    rhs=zeros[:, 0:1].to_broadcast([P, PACK * P]),
+                    start=True,
+                    stop=True,
+                )
+
+        keep_clock(4)
         transpose_tokens(0)
         quantise_tokens(0)
         for t in range(3):
+            keep_clock(1)
             transpose_corr_w(t, 0, 2, nc.scalar.copy)
             quantise_corr_w(t, 0, 2)
         first_matmul(second_psum0, 1, 0, 0)
@@ -345,18 +371,17 @@ def tile_simplemodel_pb_kernel(tc, tok, corr_w, corr_b, cross_w, cross_b, out):
             previous, multiplied = multiplied, None
             if turned > 0:
                 multiplied = (images[0:turned], multiply(codes, scales, turned))
+            if previous is not None:
+                turn_back(nc.sync if k < ROUNDS - 2 else nc.scalar, *previous)
             for slot in range(turned, len(images)):
                 direct.append((images[slot], multiply_direct(codes, scales, slot)))
-            if previous is not None:
-                turn_back(nc.scalar if k == ROUNDS - 1 else nc.sync, *previous)
             if k == 0:
                 first_psum[1] = psum_keep.tile([P, PACK, P], F32, name="first_psum1", tag="odd")
                 second_psum1 = psum.tile([P, PACK, P], F32, tag="bank")
                 for t in range(PACK):
                     first_matmul(second_psum1, 1, 1, t)
                     first_matmul(first_psum[1], 0, 1, t)
-            if k == 1:
-                second_to_sbuf(second_psum1, 1, 0, IMAGES_PER_TILE)
+                second_on_scalar(second_psum1, 1)
             if k == 3:
                 first_psum[2] = psum_keep.tile([P, PACK, P], F32, name="first_psum2v", tag="even")
                 for t in range(PACK):

@@ -178,12 +178,13 @@ def tile_simplemodel_pb_kernel(tc, tok, corr_w, corr_b, cross_w, cross_b, out):
                     op=ADD,
                 )
 
-        def second_on_scalar(product, n):
-            out_view = second[:, n * IMAGES_PER_TILE : (n + 1) * IMAGES_PER_TILE]
+        def second_on_scalar(product, n, first_image, images):
+            tokens = slice(first_image * TOKENS, (first_image + images) * TOKENS)
+            b0 = n * IMAGES_PER_TILE + first_image
             for t in range(PACK):
                 nc.scalar.activation(
-                    out=out_view[:, :, :, :, t],
-                    in_=product[:, t, :].rearrange("q (b m c) -> q b c m", m=PAIRS, c=2),
+                    out=second[:, b0 : b0 + images, :, :, t],
+                    in_=product[:, t, tokens].rearrange("q (b m c) -> q b c m", m=PAIRS, c=2),
                     func=IDENTITY,
                     bias=bias1[:, t : t + 1],
                     scale=1.0,
@@ -219,22 +220,13 @@ def tile_simplemodel_pb_kernel(tc, tok, corr_w, corr_b, cross_w, cross_b, out):
         for t in range(1, 3):
             first_matmul(second_psum0, 1, 0, t)
             first_matmul(first_psum[0], 0, 0, t)
-        transpose_tokens(2)
-        transpose_tokens(1)
-        quantise_tokens(2)
-        quantise_tokens(1)
         first_matmul(second_psum0, 1, 0, 3)
         first_matmul(first_psum[0], 0, 0, 3)
         second_to_sbuf(second_psum0, 0, 0, VECTOR_ROUNDS[0])
+        transpose_tokens(2)
+        transpose_tokens(1)
         for t in range(PACK):
             transpose_cross_w(t)
-
-        second_psum2 = psum.tile([P, PACK, P], F32, tag="bank")
-        first_psum2 = psum.tile([P, PACK, P], F32, tag="bank")
-        for t in range(PACK):
-            first_matmul(second_psum2, 1, 2, t)
-            first_matmul(first_psum2, 0, 2, t)
-        nc.scalar.copy(out=first_sbuf[:], in_=first_psum2[:].rearrange("q t r -> q r t"))
 
         def add(engine, first, b0, images, c, h_grouped):
             full = [P, images, TOKENS, PAIRS, PACK]
@@ -286,21 +278,19 @@ def tile_simplemodel_pb_kernel(tc, tok, corr_w, corr_b, cross_w, cross_b, out):
         def store_image(queue, b, result):
             queue.dma_start(out=out_rows[b * P : (b + 1) * P, :], in_=result[:])
 
-        def turn_back(queue, images, out_t):
-            for slot, b in enumerate(images):
-                back = psum.tile([P, PACK, P], F32, tag="bank")
-                for t in range(PACK):
-                    nc.tensor.transpose(back[:, t, :], out_t[:, t, slot * P : (slot + 1) * P], ident[:])
-                result = out_pool.tile([P, E], F32)
-                nc.scalar.copy(
-                    out=result[:].rearrange("i (r t) -> i r t", t=PACK),
-                    in_=back[:].rearrange("i t r -> i r t"),
-                )
-                store_image(queue, b, result)
+        def turn_back(queue, b, slot, out_t):
+            back = psum.tile([P, PACK, P], F32, tag="bank")
+            for t in range(PACK):
+                nc.tensor.transpose(back[:, t, :], out_t[:, t, slot * P : (slot + 1) * P], ident[:])
+            result = out_pool.tile([P, E], F32)
+            nc.scalar.copy(
+                out=result[:].rearrange("i (r t) -> i r t", t=PACK),
+                in_=back[:].rearrange("i t r -> i r t"),
+            )
+            store_image(queue, b, result)
 
-        def multiply_direct(codes, scales, slot):
+        def multiply_direct(codes, scales, slot, acc):
             rows = slice(slot * P, (slot + 1) * P)
-            acc = psum.tile([P, PACK, P], F32, tag="bank")
             for c in range(2):
                 nc.tensor.matmul_mx(
                     out=acc[:].rearrange("i t r -> i (t r)"),
@@ -311,7 +301,6 @@ def tile_simplemodel_pb_kernel(tc, tok, corr_w, corr_b, cross_w, cross_b, out):
                     start=(c == 0),
                     stop=(c == 1),
                 )
-            return acc
 
         def store_direct(b, acc):
             result = out_pool.tile([P, E], F32, tag="direct")
@@ -323,7 +312,7 @@ def tile_simplemodel_pb_kernel(tc, tok, corr_w, corr_b, cross_w, cross_b, out):
             )
             store_image(nc.sync, b, result)
 
-        multiplied = None
+        multiplied = []
         direct = []
         v0, g0 = 0, VECTOR_IMAGES
         for k in range(ROUNDS):
@@ -345,11 +334,24 @@ def tile_simplemodel_pb_kernel(tc, tok, corr_w, corr_b, cross_w, cross_b, out):
                     count = min(len(vector_images) - slot, IMAGES_PER_TILE - b % IMAGES_PER_TILE)
                     add_on_vector(b, count, c, h_grouped[:, slot : slot + count])
                     slot += count
-            for b, acc in direct:
+                if k == 0:
+                    quantise_tokens(2 - c)
+                if k == 0 and c == 0:
+                    second_psum2 = psum.tile([P, PACK, P], F32, tag="bank")
+                    first_psum2 = psum.tile([P, PACK, P], F32, tag="bank")
+                    for t in range(PACK):
+                        first_matmul(second_psum2, 1, 2, t)
+                        first_matmul(first_psum2, 0, 2, t)
+                    nc.scalar.copy(out=first_sbuf[:], in_=first_psum2[:].rearrange("q t r -> q r t"))
+            for b, acc in direct[0 : len(direct) // 2]:
                 store_direct(b, acc)
-            direct = []
+            direct = direct[len(direct) // 2 :]
             if k == 0:
+                gpsimd_slot = VECTOR_IMAGES % IMAGES_PER_TILE
+                second_to_sbuf(second_psum2, 2, 0, gpsimd_slot + 1)
+                second_on_scalar(second_psum2, 2, gpsimd_slot + 1, IMAGES_PER_TILE - gpsimd_slot - 1)
                 quantise_cross_w(0)
+                quantise_cross_w(1)
             codes, scales = [], []
             for c in range(2):
                 h_codes = code_pool.tile([P, ROUND * P], U32, align_bytes=64)
@@ -362,26 +364,33 @@ def tile_simplemodel_pb_kernel(tc, tok, corr_w, corr_b, cross_w, cross_b, out):
                 codes.append(h_codes)
                 scales.append(h_scales)
             if k == 0:
-                quantise_cross_w(1)
-                second_to_sbuf(second_psum2, 2, 0, IMAGES_PER_TILE)
                 second_to_sbuf(
                     second_psum0, 0, VECTOR_ROUNDS[0], IMAGES_PER_TILE - VECTOR_ROUNDS[0]
                 )
             turned = len(images) if k < ROUNDS - 2 else 0
-            previous, multiplied = multiplied, None
             if turned > 0:
-                multiplied = (images[0:turned], multiply(codes, scales, turned))
-            if previous is not None:
-                turn_back(nc.sync if k < ROUNDS - 2 else nc.scalar, *previous)
+                out_t = multiply(codes, scales, turned)
+                for slot in range(turned):
+                    multiplied.append((images[slot], slot, out_t))
+            kept = 2 if k < ROUNDS - 2 else 0
+            turn_now = max(len(multiplied) - kept, 0)
+            for b, slot, out_t in multiplied[0:turn_now]:
+                turn_back(nc.sync if k < ROUNDS - 2 else nc.scalar, b, slot, out_t)
+            multiplied = multiplied[turn_now:]
             for slot in range(turned, len(images)):
-                direct.append((images[slot], multiply_direct(codes, scales, slot)))
+                if k == ROUNDS - 1:
+                    acc = psum_keep.tile([P, PACK, P], F32, name="acc", tag=("odd", "even")[slot])
+                else:
+                    acc = psum.tile([P, PACK, P], F32, tag="bank")
+                multiply_direct(codes, scales, slot, acc)
+                direct.append((images[slot], acc))
             if k == 0:
                 first_psum[1] = psum_keep.tile([P, PACK, P], F32, name="first_psum1", tag="odd")
                 second_psum1 = psum.tile([P, PACK, P], F32, tag="bank")
                 for t in range(PACK):
                     first_matmul(second_psum1, 1, 1, t)
                     first_matmul(first_psum[1], 0, 1, t)
-                second_on_scalar(second_psum1, 1)
+                second_on_scalar(second_psum1, 1, 0, IMAGES_PER_TILE)
             if k == 3:
                 first_psum[2] = psum_keep.tile([P, PACK, P], F32, name="first_psum2v", tag="even")
                 for t in range(PACK):

@@ -207,17 +207,15 @@ def tile_simplemodel_pb_kernel(tc, tok, corr_w, corr_b, cross_w, cross_b, out):
         keep_clock(4)
         transpose_tokens(0)
         quantise_tokens(0)
-        for t in range(3):
+        for t in range(PACK):
             keep_clock(1)
-            transpose_corr_w(t, 0, 2, nc.scalar.copy)
-            quantise_corr_w(t, 0, 2)
-        first_matmul(second_psum0, 1, 0, 0)
-        first_matmul(first_psum[0], 0, 0, 0)
-        transpose_corr_w(3, 1, 1, nc.scalar.copy)
-        transpose_corr_w(3, 0, 1, nc.vector.tensor_copy)
-        quantise_corr_w(3, 1, 1)
-        quantise_corr_w(3, 0, 1)
-        for t in range(1, 3):
+            transpose_corr_w(t, 1, 1, nc.scalar.copy)
+            transpose_corr_w(t, 0, 1, nc.vector.tensor_copy)
+            if t > 0:
+                quantise_corr_w(t - 1, 0, 2)
+        quantise_corr_w(PACK - 1, 1, 1)
+        quantise_corr_w(PACK - 1, 0, 1)
+        for t in range(PACK - 1):
             first_matmul(second_psum0, 1, 0, t)
             first_matmul(first_psum[0], 0, 0, t)
         first_matmul(second_psum0, 1, 0, 3)
@@ -347,6 +345,9 @@ def tile_simplemodel_pb_kernel(tc, tok, corr_w, corr_b, cross_w, cross_b, out):
                 store_direct(b, acc)
             direct = direct[len(direct) // 2 :]
             if k == 0:
+                second_to_sbuf(
+                    second_psum0, 0, VECTOR_ROUNDS[0], IMAGES_PER_TILE - VECTOR_ROUNDS[0]
+                )
                 gpsimd_slot = VECTOR_IMAGES % IMAGES_PER_TILE
                 second_to_sbuf(second_psum2, 2, 0, gpsimd_slot + 1)
                 second_on_scalar(second_psum2, 2, gpsimd_slot + 1, IMAGES_PER_TILE - gpsimd_slot - 1)
@@ -363,10 +364,6 @@ def tile_simplemodel_pb_kernel(tc, tok, corr_w, corr_b, cross_w, cross_b, out):
                 )
                 codes.append(h_codes)
                 scales.append(h_scales)
-            if k == 0:
-                second_to_sbuf(
-                    second_psum0, 0, VECTOR_ROUNDS[0], IMAGES_PER_TILE - VECTOR_ROUNDS[0]
-                )
             turned = len(images) if k < ROUNDS - 2 else 0
             if turned > 0:
                 out_t = multiply(codes, scales, turned)

from contextlib import ExitStack

import concourse.mybir as mybir
from concourse.masks import make_identity

F32 = mybir.dt.float32
BF16 = mybir.dt.bfloat16
U32 = mybir.dt.uint32
U8 = mybir.dt.uint8
FP8X4 = mybir.dt.float8_e4m3fn_x4
ADD = mybir.AluOpType.add
IDENTITY = mybir.ActivationFunctionType.Identity

P = 128
IMAGES = 24
TOKENS = 16
PAIRS = TOKENS // 2
E = 512
PACK = 4
K_PASS = P * PACK
TOKEN_TILES = IMAGES * TOKENS // P
IMAGES_PER_TILE = P // TOKENS
ROUND = 4
VECTOR_ROUNDS = [2, 3, 3, 3, 3, 3, 1]
GPSIMD_ROUNDS = [0, 1, 1, 1, 1, 1, 1]
ROUNDS = len(VECTOR_ROUNDS)
VECTOR_IMAGES = sum(VECTOR_ROUNDS)

FLOPS = 2 * IMAGES * TOKENS * TOKENS * 2 * E * E + 2 * IMAGES * TOKENS * PAIRS * 2 * E * E


def tile_simplemodel_pb_kernel(tc, tok, corr_w, corr_b, cross_w, cross_b, out):
    nc = tc.nc
    tok_rows = tok.flatten_outer_dims()
    out_rows = out.flatten_outer_dims()

    with ExitStack() as stack:
        stack.enter_context(tc.manual_schedule())
        keep = stack.enter_context(tc.tile_pool(name="keep", bufs=1))
        h_pool = stack.enter_context(tc.tile_pool(name="h", bufs=1))
        code_pool = stack.enter_context(tc.tile_pool(name="codes", bufs=4))
        out_pool = stack.enter_context(tc.tile_pool(name="o", bufs=6))
        psum_keep = stack.enter_context(tc.psum_pool(name="psum_keep", bufs=1))
        psum = stack.enter_context(tc.psum_pool(name="psum", bufs=6))

        tok_sb = keep.tile([P, TOKEN_TILES * E], BF16)
        tok_view = tok_sb[:].rearrange("p (n k) -> p n k", n=TOKEN_TILES)
        tok_dram = tok_rows.rearrange("(n p) k -> p n k", p=P)
        nc.sync.dma_start(out=tok_view[:, 0:1], in_=tok_dram[:, 0:1])
        w1_sb = keep.tile([P, PACK * 2 * E], BF16)
        w1_dram = corr_w.rearrange("(p t) k -> t p k", t=PACK)
        for t in range(PACK):
            nc.sync.dma_start(
                out=w1_sb[:, t * 2 * E : (t + 1) * 2 * E], in_=w1_dram[t]
            )
        nc.sync.dma_start(out=tok_view[:, 1:], in_=tok_dram[:, 1:])
        w2_sb = keep.tile([P, PACK * 2 * E], BF16)
        w2_dram = cross_w.rearrange("(p t) k -> p t k", t=PACK)
        for half in range(2):
            nc.sync.dma_start(
                out=w2_sb[:, half * 4 * E : (half + 1) * 4 * E].rearrange("p (t k) -> p t k", t=2),
                in_=w2_dram[:, 2 * half : 2 * half + 2, :],
            )
        bias2_row = keep.tile([P, E], BF16)
        nc.sync.dma_start(out=bias2_row[:], in_=cross_b.partition_broadcast(P))
        bias1 = keep.tile([P, PACK], BF16)
        nc.scalar.dma_start(out=bias1[:], in_=corr_b.rearrange("(p t) -> p t", t=PACK))
        bias2 = keep.tile([P, PACK], BF16)
        nc.scalar.dma_start(out=bias2[:], in_=cross_b.rearrange("(p t) -> p t", t=PACK))

        zeros = keep.tile([P, P], BF16)
        nc.vector.memset(zeros[:], 0.0)
        ident = keep.tile([P, P], F32)
        make_identity(nc, ident[:])
        table_loaded = keep.tile([P, 1], F32)
        nc.scalar.activation(out=table_loaded[:], in_=ident[:, 0:1], func=IDENTITY)

        tok_grouped = keep.tile([P, TOKEN_TILES * P * PACK], BF16, align_bytes=64)
        tok_codes = keep.tile([P, TOKEN_TILES * P], U32, align_bytes=64)
        tok_scales = keep.tile([P, TOKEN_TILES * P], U8, align_bytes=64)
        w1_grouped = keep.tile([P, PACK * 2 * K_PASS], BF16, align_bytes=64)
        w1_codes = keep.tile([P, PACK * 2 * P], U32, align_bytes=64)
        w1_scales = keep.tile([P, PACK * 2 * P], U8, align_bytes=64)
        w2_grouped = keep.tile([P, 2 * E * PACK], BF16, align_bytes=64)
        w2_codes = keep.tile([P, 2 * E], U32, align_bytes=64)
        w2_scales = keep.tile([P, 2 * E], U8, align_bytes=64)
        second = keep.tile([P, IMAGES, 2, PAIRS, PACK], F32)
        first_sbuf = keep.tile([P, P, PACK], F32)

        def transpose_words(words, first_word, passes):
            bank = psum.tile([P, 2 * passes, P], F32, tag="bank")
            for s in range(2 * passes):
                begin = first_word + (s // 2) * 2 * P
                nc.tensor.transpose(
                    bank[:, s, :], words[:, begin + s % 2 : begin + 2 * P : 2], ident[:]
                )
            return bank

        tok_words = tok_sb[:].bitcast(F32)
        w1_words = w1_sb[:].bitcast(F32)
        w2_words = w2_sb[:].bitcast(F32)

        def transpose_tokens(n):
            bank = transpose_words(tok_words, n * 2 * P, 1)
            nc.scalar.copy(
                out=tok_grouped[:, n * K_PASS : (n + 1) * K_PASS]
                .bitcast(F32)
                .rearrange("q (r u) -> q r u", u=2),
                in_=bank[:].rearrange("q u r -> q r u"),
            )

        def quantise_tokens(n):
            nc.vector.quantize_mx(
                out=tok_codes[:, n * P : (n + 1) * P].bitcast(FP8X4),
                scales=tok_scales[:, n * P : (n + 1) * P],
                in_=tok_grouped[:, n * K_PASS : (n + 1) * K_PASS],
            )

        def transpose_corr_w(t, half, halves, copy):
            bank = transpose_words(w1_words, t * E + half * 2 * P, halves)
            start = (2 * t + half) * K_PASS
            copy(
                out=w1_grouped[:, start : start + halves * K_PASS]
                .bitcast(F32)
                .rearrange("q (h r u) -> q h r u", h=halves, u=2),
                in_=bank[:].rearrange("q (h u) r -> q h r u", u=2),
            )

        def quantise_corr_w(t, half, halves):
            start = (2 * t + half) * P
            stop = start + halves * P
            nc.vector.quantize_mx(
                out=w1_codes[:, start:stop].bitcast(FP8X4),
                scales=w1_scales[:, start:stop],
                in_=w1_grouped[:, start * PACK : stop * PACK],
            )

        def transpose_cross_w(t):
            bank = transpose_words(w2_words, t * E, 2)
            nc.scalar.copy(
                out=w2_grouped[:]
                .bitcast(F32)
                .rearrange("q (c t r u) -> q t c r u", c=2, t=PACK, u=2)[:, t],
                in_=bank[:].rearrange("q (c u) r -> q c r u", u=2),
            )

        def quantise_cross_w(pair):
            for c in range(2):
                start = c * E + pair * 2 * P
                stop = start + 2 * P
                nc.vector.quantize_mx(
                    out=w2_codes[:, start:stop].bitcast(FP8X4),
                    scales=w2_scales[:, start:stop],
                    in_=w2_grouped[:, start * PACK : stop * PACK],
                )

        def first_matmul(product, half, n, t):
            w_cols = slice((2 * t + half) * P, (2 * t + half + 1) * P)
            t_cols = slice(n * P, (n + 1) * P)
            nc.tensor.matmul_mx(
                out=product[:, t, :],
                lhsT=w1_codes[:, w_cols].bitcast(FP8X4),
                lhsT_scale=w1_scales[:, w_cols],
                rhs=tok_codes[:, t_cols].bitcast(FP8X4),
                rhs_scale=tok_scales[:, t_cols],
                start=True,
                stop=True,
            )

        def second_to_sbuf(product, n, first_image, images):
            tokens = slice(first_image * TOKENS, (first_image + images) * TOKENS)
            b0 = n * IMAGES_PER_TILE + first_image
            for c in range(2):
                nc.vector.tensor_tensor(
                    out=second[:, b0 : b0 + images, c],
                    in0=product[:, :, tokens].rearrange("q t (b m c) -> q c b m t", m=PAIRS, c=2)[:, c],
                    in1=bias1[:].unsqueeze(1).unsqueeze(1).to_broadcast([P, images, PAIRS, PACK]),
                    op=ADD,
                )

        def second_on_scalar(product, n, first_image, images):
            tokens = slice(first_image * TOKENS, (first_image + images) * TOKENS)
            b0 = n * IMAGES_PER_TILE + first_image
            for t in range(PACK):
                nc.scalar.activation(
                    out=second[:, b0 : b0 + images, :, :, t],
                    in_=product[:, t, tokens].rearrange("q (b m c) -> q b c m", m=PAIRS, c=2),
                    func=IDENTITY,
                    bias=bias1[:, t : t + 1],
                    scale=1.0,
                )

        first_psum = {}
        first_psum[0] = psum_keep.tile([P, PACK, P], F32, name="first_psum0", tag="even")
        second_psum0 = psum_keep.tile([P, PACK, P], F32, name="second_psum0", tag="odd")

        def keep_clock(passes):
            for n in range(passes):
                nc.tensor.matmul(
                    first_psum[0][:].rearrange("q t r -> q (t r)"),
                    lhsT=zeros[:],
                    rhs=zeros[:, 0:1].to_broadcast([P, PACK * P]),
                    start=True,
                    stop=True,
                )

        keep_clock(4)
        transpose_tokens(0)
        quantise_tokens(0)
        for t in range(PACK):
            keep_clock(1)
            transpose_corr_w(t, 1, 1, nc.scalar.copy)
            transpose_corr_w(t, 0, 1, nc.vector.tensor_copy)
            if t > 0:
                quantise_corr_w(t - 1, 0, 2)
        quantise_corr_w(PACK - 1, 1, 1)
        quantise_corr_w(PACK - 1, 0, 1)
        for t in range(PACK - 1):
            first_matmul(second_psum0, 1, 0, t)
            first_matmul(first_psum[0], 0, 0, t)
        first_matmul(second_psum0, 1, 0, 3)
        first_matmul(first_psum[0], 0, 0, 3)
        second_to_sbuf(second_psum0, 0, 0, VECTOR_ROUNDS[0])
        transpose_tokens(2)
        transpose_tokens(1)
        for t in range(PACK):
            transpose_cross_w(t)

        def add(engine, first, b0, images, c, h_grouped):
            full = [P, images, TOKENS, PAIRS, PACK]
            engine.tensor_tensor(
                out=h_grouped.rearrange("q b (i m t) -> q b i m t", i=TOKENS, m=PAIRS),
                in0=first.unsqueeze(3).to_broadcast(full),
                in1=second[:, b0 : b0 + images, c].unsqueeze(2).to_broadcast(full),
                op=ADD,
            )

        def add_on_vector(b0, images, c, h_grouped):
            t0 = (b0 % IMAGES_PER_TILE) * TOKENS
            bank = first_psum[b0 // IMAGES_PER_TILE]
            first = bank[:, :, t0 : t0 + images * TOKENS].rearrange("q t (b i) -> q b i t", b=images)
            add(nc.vector, first, b0, images, c, h_grouped)

        def add_on_gpsimd(b, c, h_grouped):
            t0 = (b % IMAGES_PER_TILE) * TOKENS
            first = first_sbuf[:, t0 : t0 + TOKENS, :].unsqueeze(1)
            add(nc.gpsimd, first, b, 1, c, h_grouped)

        def multiply(codes, scales, count):
            rows = slice(0, count * P)
            out_t = out_pool.tile([P, PACK, ROUND * P], F32, bufs=2)
            for t0 in range(0, PACK, ROUND // count):
                acc = psum.tile([P, ROUND // count, count * P], F32, tag="bank")
                for s in range(ROUND // count):
                    for c in range(2):
                        w_cols = slice(c * E + (t0 + s) * P, c * E + (t0 + s + 1) * P)
                        nc.tensor.matmul_mx(
                            out=acc[:, s, :],
                            lhsT=w2_codes[:, w_cols].bitcast(FP8X4),
                            lhsT_scale=w2_scales[:, w_cols],
                            rhs=codes[c][:, rows].bitcast(FP8X4),
                            rhs_scale=scales[c][:, rows],
                            start=(c == 0),
                            stop=(c == 1),
                        )
                for s in range(ROUND // count):
                    nc.scalar.activation(
                        out=out_t[:, t0 + s, rows],
                        in_=acc[:, s, :],
                        func=IDENTITY,
                        bias=bias2[:, t0 + s : t0 + s + 1],
                        scale=1.0,
                    )
            return out_t

        def store_image(queue, b, result):
            queue.dma_start(out=out_rows[b * P : (b + 1) * P, :], in_=result[:])

        def turn_back(queue, b, slot, out_t):
            back = psum.tile([P, PACK, P], F32, tag="bank")
            for t in range(PACK):
                nc.tensor.transpose(back[:, t, :], out_t[:, t, slot * P : (slot + 1) * P], ident[:])
            result = out_pool.tile([P, E], F32)
            nc.scalar.copy(
                out=result[:].rearrange("i (r t) -> i r t", t=PACK),
                in_=back[:].rearrange("i t r -> i r t"),
            )
            store_image(queue, b, result)

        def multiply_direct(codes, scales, slot, acc):
            rows = slice(slot * P, (slot + 1) * P)
            for c in range(2):
                nc.tensor.matmul_mx(
                    out=acc[:].rearrange("i t r -> i (t r)"),
                    lhsT=codes[c][:, rows].bitcast(FP8X4),
                    lhsT_scale=scales[c][:, rows],
                    rhs=w2_codes[:, c * E : (c + 1) * E].bitcast(FP8X4),
                    rhs_scale=w2_scales[:, c * E : (c + 1) * E],
                    start=(c == 0),
                    stop=(c == 1),
                )

        def store_direct(b, acc):
            result = out_pool.tile([P, E], F32, tag="direct")
            nc.vector.tensor_tensor(
                out=result[:].rearrange("i (r t) -> i r t", t=PACK),
                in0=acc[:].rearrange("i t r -> i r t"),
                in1=bias2_row[:].rearrange("i (r t) -> i r t", t=PACK),
                op=ADD,
            )
            store_image(nc.sync, b, result)

        multiplied = []
        direct = []
        v0, g0 = 0, VECTOR_IMAGES
        for k in range(ROUNDS):
            vector_images = [v0 + i for i in range(VECTOR_ROUNDS[k])]
            gpsimd_images = [g0 + i for i in range(GPSIMD_ROUNDS[k])]
            v0 += VECTOR_ROUNDS[k]
            g0 += GPSIMD_ROUNDS[k]
            images = vector_images + gpsimd_images
            h_tiles = []
            for c in range(2):
                h_grouped = h_pool.tile([P, ROUND, P * PACK], BF16, align_bytes=64, name="h%d" % c)
                h_tiles.append(h_grouped)
                for slot, b in enumerate(images):
                    if b in gpsimd_images:
                        add_on_gpsimd(b, c, h_grouped[:, slot : slot + 1])
                slot = 0
                while slot < len(vector_images):
                    b = vector_images[slot]
                    count = min(len(vector_images) - slot, IMAGES_PER_TILE - b % IMAGES_PER_TILE)
                    add_on_vector(b, count, c, h_grouped[:, slot : slot + count])
                    slot += count
                if k == 0:
                    quantise_tokens(2 - c)
                if k == 0 and c == 0:
                    second_psum2 = psum.tile([P, PACK, P], F32, tag="bank")
                    first_psum2 = psum.tile([P, PACK, P], F32, tag="bank")
                    for t in range(PACK):
                        first_matmul(second_psum2, 1, 2, t)
                        first_matmul(first_psum2, 0, 2, t)
                    nc.scalar.copy(out=first_sbuf[:], in_=first_psum2[:].rearrange("q t r -> q r t"))
            for b, acc in direct[0 : len(direct) // 2]:
                store_direct(b, acc)
            direct = direct[len(direct) // 2 :]
            if k == 0:
                second_to_sbuf(
                    second_psum0, 0, VECTOR_ROUNDS[0], IMAGES_PER_TILE - VECTOR_ROUNDS[0]
                )
                gpsimd_slot = VECTOR_IMAGES % IMAGES_PER_TILE
                second_to_sbuf(second_psum2, 2, 0, gpsimd_slot + 1)
                second_on_scalar(second_psum2, 2, gpsimd_slot + 1, IMAGES_PER_TILE - gpsimd_slot - 1)
                quantise_cross_w(0)
                quantise_cross_w(1)
            codes, scales = [], []
            for c in range(2):
                h_codes = code_pool.tile([P, ROUND * P], U32, align_bytes=64)
                h_scales = code_pool.tile([P, ROUND * P], U8, align_bytes=64)
                nc.vector.quantize_mx(
                    out=h_codes[:, 0 : len(images) * P].bitcast(FP8X4),
                    scales=h_scales[:, 0 : len(images) * P],
                    in_=h_tiles[c][:, 0 : len(images)].rearrange("q b x -> q (b x)"),
                )
                codes.append(h_codes)
                scales.append(h_scales)
            turned = len(images) if k < ROUNDS - 2 else 0
            if turned > 0:
                out_t = multiply(codes, scales, turned)
                for slot in range(turned):
                    multiplied.append((images[slot], slot, out_t))
            kept = 2 if k < ROUNDS - 2 else 0
            turn_now = max(len(multiplied) - kept, 0)
            for b, slot, out_t in multiplied[0:turn_now]:
                turn_back(nc.sync if k < ROUNDS - 2 else nc.scalar, b, slot, out_t)
            multiplied = multiplied[turn_now:]
            for slot in range(turned, len(images)):
                if k == ROUNDS - 1:
                    acc = psum_keep.tile([P, PACK, P], F32, name="acc", tag=("odd", "even")[slot])
                else:
                    acc = psum.tile([P, PACK, P], F32, tag="bank")
                multiply_direct(codes, scales, slot, acc)
                direct.append((images[slot], acc))
            if k == 0:
                first_psum[1] = psum_keep.tile([P, PACK, P], F32, name="first_psum1", tag="odd")
                second_psum1 = psum.tile([P, PACK, P], F32, tag="bank")
                for t in range(PACK):
                    first_matmul(second_psum1, 1, 1, t)
                    first_matmul(first_psum[1], 0, 1, t)
                second_on_scalar(second_psum1, 1, 0, IMAGES_PER_TILE)
            if k == 3:
                first_psum[2] = psum_keep.tile([P, PACK, P], F32, name="first_psum2v", tag="even")
                for t in range(PACK):
                    first_matmul(first_psum[2], 0, 2, t)
        for b, acc in direct:
            store_direct(b, acc)
